import numpy as np
import ml_dtypes


def mxq(x, axis, fmt="e4m3"):
    dtype, down = {"e4m3": (ml_dtypes.float8_e4m3fn, 7), "e5m2": (ml_dtypes.float8_e5m2, 14)}[fmt]
    v = np.moveaxis(np.asarray(x, np.float32).astype(ml_dtypes.bfloat16).astype(np.float64), axis, -1)
    blocks = v.reshape(v.shape[:-1] + (-1, 32))
    amax = np.abs(blocks).max(-1, keepdims=True)
    byte = np.maximum(np.where(amax > 0, np.frexp(amax)[1] - 1 + 127, 0) - down, 1)
    scale = np.exp2(byte - 127.0)
    codes = (blocks / scale).astype(np.float32).astype(dtype).astype(np.float64)
    return np.moveaxis((codes * scale).reshape(v.shape), -1, axis)


WIDE = False


def mx_kscale(k):
    if not WIDE:
        return np.ones(k)
    levels = np.array([10, -10, 5, -5, 0])
    a = np.random.permutation(np.resize(levels, k // 512 * 4)).reshape(k // 512, 4)
    idx = np.arange(k)
    return np.exp2(a[idx // 512, idx % 128 // 32])


BF16 = ml_dtypes.bfloat16


def bf(x):
    return np.asarray(x, np.float32).astype(BF16)


def f64(x):
    return np.asarray(x).astype(np.float64)


B, T, D, H = 4, 1024, 512, 4
DH = D // H
NEG_BIG = -2.0**32 + 1.0
PAD = 0.125


def heads(t):
    return t.reshape(B, T, H, DH).transpose(2, 0, 1, 3)


def setup_inputs():
    s = mx_kscale(D)
    keep_q = np.random.random((B, T, H, 1)) >= PAD
    keep_k = np.random.random((B, T, H, 1)) >= PAD
    q = (np.random.standard_normal((B, T, H, DH)) * 1.25 * keep_q).reshape(B, T, D)
    k = (np.random.standard_normal((B, T, H, DH)) * 1.25 * keep_k).reshape(B, T, D)
    return {"Q": bf(q), "K": bf(k),
            "x": bf(np.random.standard_normal((B, T, D)) * s),
            "Wv": bf(np.random.standard_normal((D, D)) / np.sqrt(D) / s[None, :]),
            "mask": bf(np.random.random((B, T)) >= 0.2)}


def reference(Q, K, x, Wv, mask):
    Qh, Kh = heads(f64(Q)), heads(f64(K))
    V = mxq(f64(x), 2, "e4m3") @ mxq(f64(Wv), 1, "e4m3").T
    Vh = heads(V)
    scores = Qh @ Kh.transpose(0, 1, 3, 2) / np.sqrt(DH)
    key_masks = np.sign(np.abs(Kh).sum(-1))
    scores = np.where(key_masks[:, :, None, :] == 0, NEG_BIG, scores)
    dir_mask = np.triu(np.ones((T, T)), 1)
    scores = scores + (1.0 - dir_mask) * -10000.0
    e = np.exp(scores - scores.max(-1, keepdims=True))
    query_masks = np.sign(np.abs(Qh).sum(-1))
    out = (mxq(e, 3, "e4m3") @ mxq(Vh, 2, "e4m3")) / e.sum(-1, keepdims=True) * query_masks[..., None]
    out = out.transpose(1, 2, 0, 3).reshape(B, T, D)
    return out * f64(mask)[:, :, None]

@@ -1,0 +1,286 @@
+import math
+from contextlib import ExitStack
+
+import concourse.mybir as mybir
+from concourse.masks import make_identity
+
+F32 = mybir.dt.float32
+BF16 = mybir.dt.bfloat16
+U32 = mybir.dt.uint32
+U8 = mybir.dt.uint8
+I32 = mybir.dt.int32
+FP8X4 = mybir.dt.float8_e4m3fn_x4
+ALU = mybir.AluOpType
+ACT = mybir.ActivationFunctionType
+AX = mybir.AxisListType
+
+B, T, D, H = 4, 1024, 512, 4
+DH = D // H
+P = 128
+PACK = 4
+K_PASS = P * PACK
+TILES = T // P
+PASSES = T // K_PASS
+BANK = 512
+BANKS_PER_ROW = T // BANK
+TILES_PER_BANK = BANK // P
+
+SCALE = 1.0 / math.sqrt(DH)
+ABSENT_KEY = (-(2.0**32) + 1.0) / SCALE
+PAST_KEY = -round(10000.0 / SCALE * 128.0) / 128.0
+
+MAGNITUDE_BITS = 0x7FFF7FFF
+
+FLOPS = 2 * B * T * D * D + 2 * 2 * B * H * T * T * DH
+
+
+def tile_multiheadattention_pa_t_kernel(tc, Q, K, x, Wv, mask, out):
+    nc = tc.nc
+    with ExitStack() as ctx:
+        const = ctx.enter_context(tc.tile_pool(name="const", bufs=1))
+        loads = ctx.enter_context(tc.tile_pool(name="loads", bufs=2))
+        batch = ctx.enter_context(tc.tile_pool(name="batch", bufs=2))
+        head = ctx.enter_context(tc.tile_pool(name="head", bufs=2))
+        rows = ctx.enter_context(tc.tile_pool(name="rows", bufs=3))
+        scratch = ctx.enter_context(tc.tile_pool(name="scratch", bufs=1))
+        ps_s = ctx.enter_context(tc.psum_pool(name="ps_s", bufs=4))
+        ps_t = ctx.enter_context(tc.psum_pool(name="ps_t", bufs=2))
+        ps_o = ctx.enter_context(tc.psum_pool(name="ps_o", bufs=2))
+
+        ident_f = const.tile([P, P], F32, name="ident_f")
+        make_identity(nc, ident_f[:])
+        ident_b = const.tile([P, P], BF16, name="ident_b")
+        make_identity(nc, ident_b[:])
+
+        past_t = const.tile([P, P], F32, name="past_t")
+        nc.gpsimd.memset(past_t[:], 0.0)
+        nc.gpsimd.affine_select(
+            out=past_t[:],
+            in_=past_t[:],
+            pattern=[[-1, P]],
+            compare_op=ALU.is_gt,
+            fill=PAST_KEY,
+            base=0,
+            channel_multiplier=1,
+        )
+
+        def words_onto_partitions(sources, grouped_words):
+            turned = ps_t.tile([P, 2, 2, P], F32, name="turned", tag="t")
+            for s in range(2):
+                words = sources[s].bitcast(F32)
+                for u in range(2):
+                    nc.tensor.transpose(out=turned[:, s, u, :], in_=words[:, u * P : (u + 1) * P], identity=ident_f[:])
+            nc.vector.tensor_copy(
+                out=grouped_words.rearrange("p (s r u) -> p s r u", s=2, u=2),
+                in_=turned[:].rearrange("p s u r -> p s r u"),
+            )
+
+        def largest_magnitude(tokens_sb, largest):
+            bits = scratch.tile([P, TILES * D // 2], I32, name="bits")
+            nc.vector.tensor_scalar(
+                out=bits[:],
+                in0=tokens_sb[:].bitcast(I32).rearrange("p c w -> p (c w)"),
+                scalar1=MAGNITUDE_BITS,
+                scalar2=None,
+                op0=ALU.bitwise_and,
+            )
+            nc.vector.tensor_reduce(
+                out=largest[:], in_=bits[:].rearrange("p (n w) -> p n w", w=DH // 2), axis=AX.X, op=ALU.max
+            )
+
+        mask_rows = const.tile([P, P], BF16, name="mask_rows")
+        nc.vector.memset(mask_rows[:], 0.0)
+        nc.sync.dma_start(out=mask_rows[0 : B * TILES, :], in_=mask.rearrange("b (r p) -> (b r) p", p=P))
+        mask_ps = ps_t.tile([P, P], BF16, name="mask_ps", tag="t")
+        nc.tensor.transpose(out=mask_ps[:], in_=mask_rows[:], identity=ident_b[:])
+        token_mask = const.tile([P, B * TILES], F32, name="token_mask")
+        nc.vector.tensor_copy(out=token_mask[:], in_=mask_ps[:, 0 : B * TILES])
+
+        w_sb = const.tile([P, H, D], BF16, name="w_sb")
+        nc.sync.dma_start(out=w_sb[:], in_=Wv.rearrange("(h p) i -> p h i", p=P))
+        w_grouped = const.tile([P, H * P * PACK], BF16, name="w_grouped", align_bytes=64)
+        for pair in range(H // 2):
+            words_onto_partitions(
+                [w_sb[:, 2 * pair, :], w_sb[:, 2 * pair + 1, :]],
+                w_grouped[:].bitcast(F32)[:, pair * BANK : (pair + 1) * BANK],
+            )
+        w_codes = const.tile([P, H * P], U32, name="w_codes", align_bytes=64)
+        w_scales = const.tile([P, H * P], U8, name="w_scales", align_bytes=64)
+        nc.vector.quantize_mx(out=w_codes[:].bitcast(FP8X4), scales=w_scales[:], in_=w_grouped[:])
+
+        for b in range(B):
+            q_sb = loads.tile([P, TILES, D], BF16, name="q_sb")
+            nc.sync.dma_start(out=q_sb[:], in_=Q[b].rearrange("(c p) d -> p c d", p=P))
+            k_sb = loads.tile([P, TILES, D], BF16, name="k_sb")
+            nc.sync.dma_start(out=k_sb[:], in_=K[b].rearrange("(c p) d -> p c d", p=P))
+            x_sb = loads.tile([P, TILES, D], BF16, name="x_sb")
+            nc.sync.dma_start(
+                out=x_sb[:].rearrange("p (a e) d -> p a (e d)", e=2),
+                in_=x[b].rearrange("(a p e) d -> p a (e d)", p=P, e=2),
+            )
+
+            x_grouped = batch.tile([P, TILES * P * PACK], BF16, name="x_grouped", align_bytes=64)
+            for pair in range(TILES // 2):
+                words_onto_partitions(
+                    [x_sb[:, 2 * pair, :], x_sb[:, 2 * pair + 1, :]],
+                    x_grouped[:].bitcast(F32)[:, pair * BANK : (pair + 1) * BANK],
+                )
+            x_codes = batch.tile([P, TILES * P], U32, name="x_codes", align_bytes=64)
+            x_scales = batch.tile([P, TILES * P], U8, name="x_scales", align_bytes=64)
+            nc.vector.quantize_mx(out=x_codes[:].bitcast(FP8X4), scales=x_scales[:], in_=x_grouped[:])
+
+            v_grouped = batch.tile([P, H * PASSES * DH * PACK], BF16, name="v_grouped", align_bytes=64)
+            for h in range(H):
+                for g in range(PASSES):
+                    v_ps = ps_o.tile([P, PACK, DH], F32, name="v_ps", tag="o")
+                    for t in range(PACK):
+                        s = PACK * g + t
+                        nc.tensor.matmul_mx(
+                            out=v_ps[:, t, :],
+                            lhsT=x_codes[:, s * P : (s + 1) * P].bitcast(FP8X4),
+                            lhsT_scale=x_scales[:, s * P : (s + 1) * P],
+                            rhs=w_codes[:, h * DH : (h + 1) * DH].bitcast(FP8X4),
+                            rhs_scale=w_scales[:, h * DH : (h + 1) * DH],
+                            start=True,
+                            stop=True,
+                        )
+                    piece = (h * PASSES + g) * DH * PACK
+                    nc.vector.tensor_copy(
+                        out=v_grouped[:, piece : piece + DH * PACK].rearrange("p (d t) -> p d t", t=PACK),
+                        in_=v_ps[:].rearrange("p t d -> p d t"),
+                    )
+            v_codes = batch.tile([P, H * PASSES * DH], U32, name="v_codes", align_bytes=64)
+            v_scales = batch.tile([P, H * PASSES * DH], U8, name="v_scales", align_bytes=64)
+            nc.vector.quantize_mx(out=v_codes[:].bitcast(FP8X4), scales=v_scales[:], in_=v_grouped[:])
+
+            k_abs = batch.tile([P, TILES * H], F32, name="k_abs")
+            largest_magnitude(k_sb, k_abs)
+            later_key = batch.tile([P, TILES * H], F32, name="later_key")
+            nc.vector.tensor_scalar(
+                out=later_key[:], in0=k_abs[:], scalar1=0.0, scalar2=ABSENT_KEY, op0=ALU.is_equal, op1=ALU.mult
+            )
+            past_key = batch.tile([P, TILES * H], F32, name="past_key")
+            nc.vector.tensor_scalar_add(out=past_key[:], in0=later_key[:], scalar1=PAST_KEY)
+
+            q_abs = batch.tile([P, TILES * H], F32, name="q_abs")
+            largest_magnitude(q_sb, q_abs)
+            row_on = batch.tile([P, TILES, H], F32, name="row_on")
+            nc.vector.tensor_scalar(
+                out=row_on[:].rearrange("p c h -> p (c h)"), in0=q_abs[:], scalar1=0.0, scalar2=None, op0=ALU.is_gt
+            )
+            nc.vector.tensor_tensor(
+                out=row_on[:],
+                in0=row_on[:],
+                in1=token_mask[:, b * TILES : (b + 1) * TILES].unsqueeze(2).to_broadcast([P, TILES, H]),
+                op=ALU.mult,
+            )
+
+            q_t = batch.tile([P, H, T], BF16, name="q_t")
+            k_t = batch.tile([P, H, T], BF16, name="k_t")
+            for h in range(H):
+                for source, turned_sb in ((q_sb, q_t), (k_sb, k_t)):
+                    turned_ps = ps_t.tile([P, T], BF16, name="turned_ps", tag="t")
+                    for c in range(TILES):
+                        nc.tensor.transpose(
+                            out=turned_ps[:, c * P : (c + 1) * P],
+                            in_=source[:, c, h * DH : (h + 1) * DH],
+                            identity=ident_b[:],
+                        )
+                    nc.scalar.copy(out=turned_sb[:, h, :], in_=turned_ps[:])
+
+            o_sb = batch.tile([P, TILES, D], F32, name="o_sb")
+            for h in range(H):
+                e_codes = head.tile([P, TILES * PASSES * P], U32, name="e_codes", align_bytes=64)
+                e_scales = head.tile([P, TILES * PASSES * P], U8, name="e_scales", align_bytes=64)
+                row_sums = head.tile([P, TILES, BANKS_PER_ROW], F32, name="row_sums")
+                for r in range(TILES):
+                    banks = []
+                    for k in range(BANKS_PER_ROW):
+                        s_ps = ps_s.tile([P, BANK], F32, name="s_ps", tag="s")
+                        banks.append(s_ps)
+                        nc.tensor.matmul(
+                            out=s_ps[:],
+                            lhsT=q_t[:, h, r * P : (r + 1) * P],
+                            rhs=k_t[:, h, k * BANK : (k + 1) * BANK],
+                            start=True,
+                            stop=False,
+                        )
+                        addends = []
+                        for c4 in range(TILES_PER_BANK):
+                            c = k * TILES_PER_BANK + c4
+                            column = past_key if c < r else later_key
+                            addends.append((c4, column[:, c * H + h : c * H + h + 1].to_broadcast([P, P])))
+                            if c == r:
+                                addends.append((c4, past_t[:]))
+                        for n, (c4, addend) in enumerate(addends):
+                            nc.tensor.matmul(
+                                out=s_ps[:, c4 * P : (c4 + 1) * P],
+                                lhsT=addend,
+                                rhs=ident_f[:],
+                                start=False,
+                                stop=(n == len(addends) - 1),
+                                is_transpose=True,
+                            )
+                    bank_max = rows.tile([P, BANKS_PER_ROW], F32, name="bank_max")
+                    for k in range(BANKS_PER_ROW):
+                        nc.vector.tensor_reduce(out=bank_max[:, k : k + 1], in_=banks[k][:], axis=AX.X, op=ALU.max)
+                    shift = rows.tile([P, 1], F32, name="shift")
+                    nc.vector.tensor_scalar(
+                        out=shift[:],
+                        in0=bank_max[:, 0:1],
+                        scalar1=bank_max[:, 1:2],
+                        scalar2=-SCALE,
+                        op0=ALU.max,
+                        op1=ALU.mult,
+                    )
+                    e_sb = rows.tile([P, T], BF16, name="e_sb")
+                    for k in range(BANKS_PER_ROW):
+                        nc.scalar.activation(
+                            out=e_sb[:, k * BANK : (k + 1) * BANK],
+                            in_=banks[k][:],
+                            func=ACT.Exp,
+                            bias=shift[:],
+                            scale=SCALE,
+                            accum_out=row_sums[:, r, k : k + 1],
+                        )
+                    e_t = ps_t.tile([P, PASSES, 2, P], F32, name="e_t", tag="t")
+                    e_words = e_sb[:].bitcast(F32)
+                    for g in range(PASSES):
+                        for u in range(2):
+                            w = 2 * g + u
+                            nc.tensor.transpose(out=e_t[:, g, u, :], in_=e_words[:, w * P : (w + 1) * P], identity=ident_f[:])
+                    e_grouped = rows.tile([P, PASSES * P * PACK], BF16, name="e_grouped", align_bytes=64)
+                    nc.scalar.copy(
+                        out=e_grouped[:].bitcast(F32).rearrange("p (g q u) -> p g q u", g=PASSES, u=2),
+                        in_=e_t[:].rearrange("p g u q -> p g q u"),
+                    )
+                    cols = slice(r * PASSES * P, (r + 1) * PASSES * P)
+                    nc.vector.quantize_mx(out=e_codes[:, cols].bitcast(FP8X4), scales=e_scales[:, cols], in_=e_grouped[:])
+
+                weight = head.tile([P, TILES], F32, name="weight")
+                nc.vector.tensor_reduce(out=weight[:], in_=row_sums[:], axis=AX.X, op=ALU.add)
+                nc.vector.reciprocal(out=weight[:], in_=weight[:])
+                nc.vector.tensor_tensor(out=weight[:], in0=weight[:], in1=row_on[:, :, h], op=ALU.mult)
+
+                for half in range(2):
+                    o_ps = ps_o.tile([P, TILES // 2, DH], F32, name="o_ps", tag="o")
+                    for r4 in range(TILES // 2):
+                        r = half * (TILES // 2) + r4
+                        for g in range(PASSES):
+                            e_cols = slice((r * PASSES + g) * P, (r * PASSES + g + 1) * P)
+                            v_cols = slice((h * PASSES + g) * DH, (h * PASSES + g + 1) * DH)
+                            nc.tensor.matmul_mx(
+                                out=o_ps[:, r4, :],
+                                lhsT=e_codes[:, e_cols].bitcast(FP8X4),
+                                lhsT_scale=e_scales[:, e_cols],
+                                rhs=v_codes[:, v_cols].bitcast(FP8X4),
+                                rhs_scale=v_scales[:, v_cols],
+                                start=(g == 0),
+                                stop=(g == PASSES - 1),
+                            )
+                    for r4 in range(TILES // 2):
+                        r = half * (TILES // 2) + r4
+                        nc.vector.tensor_scalar_mul(
+                            out=o_sb[:, r, h * DH : (h + 1) * DH], in0=o_ps[:, r4, :], scalar1=weight[:, r : r + 1]
+                        )
+            nc.sync.dma_start(out=out[b].rearrange("(r p) d -> p r d", p=P), in_=o_sb[:])

@@ -24,12 +24,23 @@ PASSES = T // K_PASS
 BANK = 512
 BANKS_PER_ROW = T // BANK
 TILES_PER_BANK = BANK // P
+GROUP = BANK // DH
+ROW_TILES = B * H * TILES
 
 SCALE = 1.0 / math.sqrt(DH)
 ABSENT_KEY = (-(2.0**32) + 1.0) / SCALE
 PAST_KEY = -round(10000.0 / SCALE * 128.0) / 128.0
-
 MAGNITUDE_BITS = 0x7FFF7FFF
+
+LAG_MAX = 1
+LAG_EXP = 2
+LAG_TURN = 3
+LAG_QUANTISE = 4
+LAG_E_TIMES_V = 5
+LAG_SUM = 3
+LAG_INVERT = 4
+LAG_WEIGH = 5
+LAG_FINISH = 6
 
 FLOPS = 2 * B * T * D * D + 2 * 2 * B * H * T * T * DH
 
@@ -38,14 +49,7 @@ def tile_multiheadattention_pa_t_kernel(tc, Q, K, x, Wv, mask, out):
     nc = tc.nc
     with ExitStack() as ctx:
         const = ctx.enter_context(tc.tile_pool(name="const", bufs=1))
-        loads = ctx.enter_context(tc.tile_pool(name="loads", bufs=2))
-        batch = ctx.enter_context(tc.tile_pool(name="batch", bufs=2))
-        head = ctx.enter_context(tc.tile_pool(name="head", bufs=2))
-        rows = ctx.enter_context(tc.tile_pool(name="rows", bufs=3))
-        scratch = ctx.enter_context(tc.tile_pool(name="scratch", bufs=1))
-        ps_s = ctx.enter_context(tc.psum_pool(name="ps_s", bufs=4))
-        ps_t = ctx.enter_context(tc.psum_pool(name="ps_t", bufs=2))
-        ps_o = ctx.enter_context(tc.psum_pool(name="ps_o", bufs=2))
+        keep = ctx.enter_context(tc.tile_pool(name="keep", bufs=1))
 
         ident_f = const.tile([P, P], F32, name="ident_f")
         make_identity(nc, ident_f[:])
@@ -64,223 +68,333 @@ def tile_multiheadattention_pa_t_kernel(tc, Q, K, x, Wv, mask, out):
             channel_multiplier=1,
         )
 
-        def words_onto_partitions(sources, grouped_words):
-            turned = ps_t.tile([P, 2, 2, P], F32, name="turned", tag="t")
-            for s in range(2):
-                words = sources[s].bitcast(F32)
-                for u in range(2):
-                    nc.tensor.transpose(out=turned[:, s, u, :], in_=words[:, u * P : (u + 1) * P], identity=ident_f[:])
-            nc.vector.tensor_copy(
-                out=grouped_words.rearrange("p (s r u) -> p s r u", s=2, u=2),
-                in_=turned[:].rearrange("p s u r -> p s r u"),
-            )
+        q_t = keep.tile([P, B, H, T], BF16, name="q_t")
+        k_t = keep.tile([P, B, H, T], BF16, name="k_t")
+        v_codes = keep.tile([P, B, H * PASSES * DH], U32, name="v_codes", align_bytes=64)
+        v_scales = keep.tile([P, B, H * PASSES * DH], U8, name="v_scales", align_bytes=64)
+        later_key = keep.tile([P, B, TILES * H], F32, name="later_key")
+        past_key = keep.tile([P, B, TILES * H], F32, name="past_key")
+        row_on = keep.tile([P, B, TILES, H], F32, name="row_on")
 
-        def largest_magnitude(tokens_sb, largest):
-            bits = scratch.tile([P, TILES * D // 2], I32, name="bits")
-            nc.vector.tensor_scalar(
-                out=bits[:],
-                in0=tokens_sb[:].bitcast(I32).rearrange("p c w -> p (c w)"),
-                scalar1=MAGNITUDE_BITS,
-                scalar2=None,
-                op0=ALU.bitwise_and,
-            )
-            nc.vector.tensor_reduce(
-                out=largest[:], in_=bits[:].rearrange("p (n w) -> p n w", w=DH // 2), axis=AX.X, op=ALU.max
-            )
+        with ExitStack() as phase:
+            loads = phase.enter_context(tc.tile_pool(name="loads", bufs=2))
+            work = phase.enter_context(tc.tile_pool(name="work", bufs=2))
+            once = phase.enter_context(tc.tile_pool(name="once", bufs=1))
+            ps_t = phase.enter_context(tc.psum_pool(name="ps_t", bufs=4))
+            ps_v = phase.enter_context(tc.psum_pool(name="ps_v", bufs=4))
 
-        mask_rows = const.tile([P, P], BF16, name="mask_rows")
-        nc.vector.memset(mask_rows[:], 0.0)
-        nc.sync.dma_start(out=mask_rows[0 : B * TILES, :], in_=mask.rearrange("b (r p) -> (b r) p", p=P))
-        mask_ps = ps_t.tile([P, P], BF16, name="mask_ps", tag="t")
-        nc.tensor.transpose(out=mask_ps[:], in_=mask_rows[:], identity=ident_b[:])
-        token_mask = const.tile([P, B * TILES], F32, name="token_mask")
-        nc.vector.tensor_copy(out=token_mask[:], in_=mask_ps[:, 0 : B * TILES])
-
-        w_sb = const.tile([P, H, D], BF16, name="w_sb")
-        nc.sync.dma_start(out=w_sb[:], in_=Wv.rearrange("(h p) i -> p h i", p=P))
-        w_grouped = const.tile([P, H * P * PACK], BF16, name="w_grouped", align_bytes=64)
-        for pair in range(H // 2):
-            words_onto_partitions(
-                [w_sb[:, 2 * pair, :], w_sb[:, 2 * pair + 1, :]],
-                w_grouped[:].bitcast(F32)[:, pair * BANK : (pair + 1) * BANK],
-            )
-        w_codes = const.tile([P, H * P], U32, name="w_codes", align_bytes=64)
-        w_scales = const.tile([P, H * P], U8, name="w_scales", align_bytes=64)
-        nc.vector.quantize_mx(out=w_codes[:].bitcast(FP8X4), scales=w_scales[:], in_=w_grouped[:])
-
-        for b in range(B):
-            q_sb = loads.tile([P, TILES, D], BF16, name="q_sb")
-            nc.sync.dma_start(out=q_sb[:], in_=Q[b].rearrange("(c p) d -> p c d", p=P))
-            k_sb = loads.tile([P, TILES, D], BF16, name="k_sb")
-            nc.sync.dma_start(out=k_sb[:], in_=K[b].rearrange("(c p) d -> p c d", p=P))
-            x_sb = loads.tile([P, TILES, D], BF16, name="x_sb")
-            nc.sync.dma_start(
-                out=x_sb[:].rearrange("p (a e) d -> p a (e d)", e=2),
-                in_=x[b].rearrange("(a p e) d -> p a (e d)", p=P, e=2),
-            )
-
-            x_grouped = batch.tile([P, TILES * P * PACK], BF16, name="x_grouped", align_bytes=64)
-            for pair in range(TILES // 2):
-                words_onto_partitions(
-                    [x_sb[:, 2 * pair, :], x_sb[:, 2 * pair + 1, :]],
-                    x_grouped[:].bitcast(F32)[:, pair * BANK : (pair + 1) * BANK],
-                )
-            x_codes = batch.tile([P, TILES * P], U32, name="x_codes", align_bytes=64)
-            x_scales = batch.tile([P, TILES * P], U8, name="x_scales", align_bytes=64)
-            nc.vector.quantize_mx(out=x_codes[:].bitcast(FP8X4), scales=x_scales[:], in_=x_grouped[:])
-
-            v_grouped = batch.tile([P, H * PASSES * DH * PACK], BF16, name="v_grouped", align_bytes=64)
-            for h in range(H):
-                for g in range(PASSES):
-                    v_ps = ps_o.tile([P, PACK, DH], F32, name="v_ps", tag="o")
-                    for t in range(PACK):
-                        s = PACK * g + t
-                        nc.tensor.matmul_mx(
-                            out=v_ps[:, t, :],
-                            lhsT=x_codes[:, s * P : (s + 1) * P].bitcast(FP8X4),
-                            lhsT_scale=x_scales[:, s * P : (s + 1) * P],
-                            rhs=w_codes[:, h * DH : (h + 1) * DH].bitcast(FP8X4),
-                            rhs_scale=w_scales[:, h * DH : (h + 1) * DH],
-                            start=True,
-                            stop=True,
-                        )
-                    piece = (h * PASSES + g) * DH * PACK
-                    nc.vector.tensor_copy(
-                        out=v_grouped[:, piece : piece + DH * PACK].rearrange("p (d t) -> p d t", t=PACK),
-                        in_=v_ps[:].rearrange("p t d -> p d t"),
-                    )
-            v_codes = batch.tile([P, H * PASSES * DH], U32, name="v_codes", align_bytes=64)
-            v_scales = batch.tile([P, H * PASSES * DH], U8, name="v_scales", align_bytes=64)
-            nc.vector.quantize_mx(out=v_codes[:].bitcast(FP8X4), scales=v_scales[:], in_=v_grouped[:])
-
-            k_abs = batch.tile([P, TILES * H], F32, name="k_abs")
-            largest_magnitude(k_sb, k_abs)
-            later_key = batch.tile([P, TILES * H], F32, name="later_key")
-            nc.vector.tensor_scalar(
-                out=later_key[:], in0=k_abs[:], scalar1=0.0, scalar2=ABSENT_KEY, op0=ALU.is_equal, op1=ALU.mult
-            )
-            past_key = batch.tile([P, TILES * H], F32, name="past_key")
-            nc.vector.tensor_scalar_add(out=past_key[:], in0=later_key[:], scalar1=PAST_KEY)
-
-            q_abs = batch.tile([P, TILES * H], F32, name="q_abs")
-            largest_magnitude(q_sb, q_abs)
-            row_on = batch.tile([P, TILES, H], F32, name="row_on")
-            nc.vector.tensor_scalar(
-                out=row_on[:].rearrange("p c h -> p (c h)"), in0=q_abs[:], scalar1=0.0, scalar2=None, op0=ALU.is_gt
-            )
-            nc.vector.tensor_tensor(
-                out=row_on[:],
-                in0=row_on[:],
-                in1=token_mask[:, b * TILES : (b + 1) * TILES].unsqueeze(2).to_broadcast([P, TILES, H]),
-                op=ALU.mult,
-            )
-
-            q_t = batch.tile([P, H, T], BF16, name="q_t")
-            k_t = batch.tile([P, H, T], BF16, name="k_t")
-            for h in range(H):
-                for source, turned_sb in ((q_sb, q_t), (k_sb, k_t)):
-                    turned_ps = ps_t.tile([P, T], BF16, name="turned_ps", tag="t")
-                    for c in range(TILES):
+            def words_onto_partitions(sources, grouped_words):
+                turned = ps_t.tile([P, 2, 2, P], F32, name="turned", tag="t")
+                for s in range(2):
+                    words = sources[s].bitcast(F32)
+                    for u in range(2):
                         nc.tensor.transpose(
-                            out=turned_ps[:, c * P : (c + 1) * P],
-                            in_=source[:, c, h * DH : (h + 1) * DH],
-                            identity=ident_b[:],
+                            out=turned[:, s, u, :], in_=words[:, u * P : (u + 1) * P], identity=ident_f[:]
                         )
-                    nc.scalar.copy(out=turned_sb[:, h, :], in_=turned_ps[:])
+                nc.scalar.copy(
+                    out=grouped_words.rearrange("p (s r u) -> p s r u", s=2, u=2),
+                    in_=turned[:].rearrange("p s u r -> p s r u"),
+                )
 
-            o_sb = batch.tile([P, TILES, D], F32, name="o_sb")
-            for h in range(H):
-                e_codes = head.tile([P, TILES * PASSES * P], U32, name="e_codes", align_bytes=64)
-                e_scales = head.tile([P, TILES * PASSES * P], U8, name="e_scales", align_bytes=64)
-                row_sums = head.tile([P, TILES, BANKS_PER_ROW], F32, name="row_sums")
-                for r in range(TILES):
-                    banks = []
-                    for k in range(BANKS_PER_ROW):
-                        s_ps = ps_s.tile([P, BANK], F32, name="s_ps", tag="s")
-                        banks.append(s_ps)
-                        nc.tensor.matmul(
-                            out=s_ps[:],
-                            lhsT=q_t[:, h, r * P : (r + 1) * P],
-                            rhs=k_t[:, h, k * BANK : (k + 1) * BANK],
-                            start=True,
-                            stop=False,
-                        )
-                        addends = []
-                        for c4 in range(TILES_PER_BANK):
-                            c = k * TILES_PER_BANK + c4
-                            column = past_key if c < r else later_key
-                            addends.append((c4, column[:, c * H + h : c * H + h + 1].to_broadcast([P, P])))
-                            if c == r:
-                                addends.append((c4, past_t[:]))
-                        for n, (c4, addend) in enumerate(addends):
-                            nc.tensor.matmul(
-                                out=s_ps[:, c4 * P : (c4 + 1) * P],
-                                lhsT=addend,
-                                rhs=ident_f[:],
-                                start=False,
-                                stop=(n == len(addends) - 1),
-                                is_transpose=True,
-                            )
-                    bank_max = rows.tile([P, BANKS_PER_ROW], F32, name="bank_max")
-                    for k in range(BANKS_PER_ROW):
-                        nc.vector.tensor_reduce(out=bank_max[:, k : k + 1], in_=banks[k][:], axis=AX.X, op=ALU.max)
-                    shift = rows.tile([P, 1], F32, name="shift")
-                    nc.vector.tensor_scalar(
-                        out=shift[:],
-                        in0=bank_max[:, 0:1],
-                        scalar1=bank_max[:, 1:2],
-                        scalar2=-SCALE,
-                        op0=ALU.max,
-                        op1=ALU.mult,
+            def largest_magnitude(tokens_sb, largest):
+                bits = once.tile([P, TILES * D // 2], I32, name="bits")
+                nc.vector.tensor_scalar(
+                    out=bits[:],
+                    in0=tokens_sb[:].bitcast(I32).rearrange("p c w -> p (c w)"),
+                    scalar1=MAGNITUDE_BITS,
+                    scalar2=None,
+                    op0=ALU.bitwise_and,
+                )
+                nc.vector.tensor_reduce(
+                    out=largest[:], in_=bits[:].rearrange("p (n w) -> p n w", w=DH // 2), axis=AX.X, op=ALU.max
+                )
+
+            mask_rows = once.tile([P, P], BF16, name="mask_rows")
+            nc.vector.memset(mask_rows[:], 0.0)
+            nc.sync.dma_start(out=mask_rows[0 : B * TILES, :], in_=mask.rearrange("b (r p) -> (b r) p", p=P))
+            w_sb = once.tile([P, H, D], BF16, name="w_sb")
+            nc.sync.dma_start(out=w_sb[:], in_=Wv.rearrange("(h p) i -> p h i", p=P))
+
+            mask_ps = ps_t.tile([P, P], BF16, name="mask_ps", tag="t")
+            nc.tensor.transpose(out=mask_ps[:], in_=mask_rows[:], identity=ident_b[:])
+            token_mask = once.tile([P, B, TILES], F32, name="token_mask")
+            nc.vector.tensor_copy(out=token_mask[:].rearrange("p b r -> p (b r)"), in_=mask_ps[:, 0 : B * TILES])
+
+            w_grouped = once.tile([P, H * P * PACK], BF16, name="w_grouped", align_bytes=64)
+            for pair in range(H // 2):
+                words_onto_partitions(
+                    [w_sb[:, 2 * pair, :], w_sb[:, 2 * pair + 1, :]],
+                    w_grouped[:].bitcast(F32)[:, pair * BANK : (pair + 1) * BANK],
+                )
+            w_codes = once.tile([P, H * P], U32, name="w_codes", align_bytes=64)
+            w_scales = once.tile([P, H * P], U8, name="w_scales", align_bytes=64)
+            nc.vector.quantize_mx(out=w_codes[:].bitcast(FP8X4), scales=w_scales[:], in_=w_grouped[:])
+
+            for b in range(B):
+                x_sb = loads.tile([P, TILES, D], BF16, name="x_sb")
+                nc.sync.dma_start(
+                    out=x_sb[:].rearrange("p (a e) d -> p a (e d)", e=2),
+                    in_=x[b].rearrange("(a p e) d -> p a (e d)", p=P, e=2),
+                )
+                k_sb = loads.tile([P, TILES, D], BF16, name="k_sb")
+                nc.sync.dma_start(out=k_sb[:], in_=K[b].rearrange("(c p) d -> p c d", p=P))
+                q_sb = loads.tile([P, TILES, D], BF16, name="q_sb")
+                nc.sync.dma_start(out=q_sb[:], in_=Q[b].rearrange("(c p) d -> p c d", p=P))
+
+                x_grouped = work.tile([P, TILES * P * PACK], BF16, name="x_grouped", align_bytes=64)
+                for pair in range(TILES // 2):
+                    words_onto_partitions(
+                        [x_sb[:, 2 * pair, :], x_sb[:, 2 * pair + 1, :]],
+                        x_grouped[:].bitcast(F32)[:, pair * BANK : (pair + 1) * BANK],
                     )
-                    e_sb = rows.tile([P, T], BF16, name="e_sb")
-                    for k in range(BANKS_PER_ROW):
-                        nc.scalar.activation(
-                            out=e_sb[:, k * BANK : (k + 1) * BANK],
-                            in_=banks[k][:],
-                            func=ACT.Exp,
-                            bias=shift[:],
-                            scale=SCALE,
-                            accum_out=row_sums[:, r, k : k + 1],
-                        )
-                    e_t = ps_t.tile([P, PASSES, 2, P], F32, name="e_t", tag="t")
-                    e_words = e_sb[:].bitcast(F32)
+
+                k_abs = work.tile([P, TILES * H], F32, name="k_abs")
+                largest_magnitude(k_sb, k_abs)
+                nc.vector.tensor_scalar(
+                    out=later_key[:, b, :], in0=k_abs[:], scalar1=0.0, scalar2=ABSENT_KEY, op0=ALU.is_equal, op1=ALU.mult
+                )
+                x_codes = work.tile([P, TILES * P], U32, name="x_codes", align_bytes=64)
+                x_scales = work.tile([P, TILES * P], U8, name="x_scales", align_bytes=64)
+                nc.vector.quantize_mx(out=x_codes[:].bitcast(FP8X4), scales=x_scales[:], in_=x_grouped[:])
+                nc.vector.tensor_scalar_add(out=past_key[:, b, :], in0=later_key[:, b, :], scalar1=PAST_KEY)
+
+                q_abs = work.tile([P, TILES * H], F32, name="q_abs")
+                largest_magnitude(q_sb, q_abs)
+                nc.vector.tensor_scalar(
+                    out=row_on[:, b, :, :].rearrange("p c h -> p (c h)"),
+                    in0=q_abs[:],
+                    scalar1=0.0,
+                    scalar2=None,
+                    op0=ALU.is_gt,
+                )
+
+                for h in range(H):
+                    for source, turned_sb in ((k_sb, k_t), (q_sb, q_t)):
+                        turned_ps = ps_t.tile([P, T], BF16, name="turned_ps", tag="t")
+                        for c in range(TILES):
+                            nc.tensor.transpose(
+                                out=turned_ps[:, c * P : (c + 1) * P],
+                                in_=source[:, c, h * DH : (h + 1) * DH],
+                                identity=ident_b[:],
+                            )
+                        nc.scalar.copy(out=turned_sb[:, b, h, :], in_=turned_ps[:])
+
+                nc.vector.tensor_tensor(
+                    out=row_on[:, b, :, :],
+                    in0=row_on[:, b, :, :],
+                    in1=token_mask[:, b, :].unsqueeze(2).to_broadcast([P, TILES, H]),
+                    op=ALU.mult,
+                )
+
+                v_grouped = work.tile([P, H * PASSES * DH * PACK], BF16, name="v_grouped", align_bytes=64)
+                for h in range(H):
                     for g in range(PASSES):
-                        for u in range(2):
-                            w = 2 * g + u
-                            nc.tensor.transpose(out=e_t[:, g, u, :], in_=e_words[:, w * P : (w + 1) * P], identity=ident_f[:])
-                    e_grouped = rows.tile([P, PASSES * P * PACK], BF16, name="e_grouped", align_bytes=64)
-                    nc.scalar.copy(
-                        out=e_grouped[:].bitcast(F32).rearrange("p (g q u) -> p g q u", g=PASSES, u=2),
-                        in_=e_t[:].rearrange("p g u q -> p g q u"),
-                    )
-                    cols = slice(r * PASSES * P, (r + 1) * PASSES * P)
-                    nc.vector.quantize_mx(out=e_codes[:, cols].bitcast(FP8X4), scales=e_scales[:, cols], in_=e_grouped[:])
-
-                weight = head.tile([P, TILES], F32, name="weight")
-                nc.vector.tensor_reduce(out=weight[:], in_=row_sums[:], axis=AX.X, op=ALU.add)
-                nc.vector.reciprocal(out=weight[:], in_=weight[:])
-                nc.vector.tensor_tensor(out=weight[:], in0=weight[:], in1=row_on[:, :, h], op=ALU.mult)
-
-                for half in range(2):
-                    o_ps = ps_o.tile([P, TILES // 2, DH], F32, name="o_ps", tag="o")
-                    for r4 in range(TILES // 2):
-                        r = half * (TILES // 2) + r4
-                        for g in range(PASSES):
-                            e_cols = slice((r * PASSES + g) * P, (r * PASSES + g + 1) * P)
-                            v_cols = slice((h * PASSES + g) * DH, (h * PASSES + g + 1) * DH)
+                        v_ps = ps_v.tile([P, PACK, DH], F32, name="v_ps", tag="v")
+                        for t in range(PACK):
+                            s = PACK * g + t
                             nc.tensor.matmul_mx(
-                                out=o_ps[:, r4, :],
-                                lhsT=e_codes[:, e_cols].bitcast(FP8X4),
-                                lhsT_scale=e_scales[:, e_cols],
-                                rhs=v_codes[:, v_cols].bitcast(FP8X4),
-                                rhs_scale=v_scales[:, v_cols],
-                                start=(g == 0),
-                                stop=(g == PASSES - 1),
+                                out=v_ps[:, t, :],
+                                lhsT=x_codes[:, s * P : (s + 1) * P].bitcast(FP8X4),
+                                lhsT_scale=x_scales[:, s * P : (s + 1) * P],
+                                rhs=w_codes[:, h * DH : (h + 1) * DH].bitcast(FP8X4),
+                                rhs_scale=w_scales[:, h * DH : (h + 1) * DH],
+                                start=True,
+                                stop=True,
                             )
-                    for r4 in range(TILES // 2):
-                        r = half * (TILES // 2) + r4
-                        nc.vector.tensor_scalar_mul(
-                            out=o_sb[:, r, h * DH : (h + 1) * DH], in0=o_ps[:, r4, :], scalar1=weight[:, r : r + 1]
+                        piece = (h * PASSES + g) * DH * PACK
+                        nc.scalar.copy(
+                            out=v_grouped[:, piece : piece + DH * PACK].rearrange("p (d t) -> p d t", t=PACK),
+                            in_=v_ps[:].rearrange("p t d -> p d t"),
                         )
-            nc.sync.dma_start(out=out[b].rearrange("(r p) d -> p r d", p=P), in_=o_sb[:])
+                nc.vector.quantize_mx(out=v_codes[:, b, :].bitcast(FP8X4), scales=v_scales[:, b, :], in_=v_grouped[:])
+
+        with ExitStack() as phase:
+            rows = phase.enter_context(tc.tile_pool(name="rows", bufs=3))
+            groups = phase.enter_context(tc.tile_pool(name="groups", bufs=3))
+            ps_s = phase.enter_context(tc.psum_pool(name="ps_s", bufs=6))
+            ps_r = phase.enter_context(tc.psum_pool(name="ps_r", bufs=2))
+            phase.enter_context(tc.manual_schedule())
+
+            tiles = {}
+
+            def where(i):
+                return i // (H * TILES), (i // TILES) % H, i % TILES
+
+            def scores(i):
+                b, h, r = where(i)
+                banks = []
+                for k in range(BANKS_PER_ROW):
+                    s_ps = ps_s.tile([P, BANK], F32, name="s_ps", tag="s")
+                    banks.append(s_ps)
+                    nc.tensor.matmul(
+                        out=s_ps[:],
+                        lhsT=q_t[:, b, h, r * P : (r + 1) * P],
+                        rhs=k_t[:, b, h, k * BANK : (k + 1) * BANK],
+                        start=True,
+                        stop=False,
+                    )
+                for k in range(BANKS_PER_ROW):
+                    addends = []
+                    for c4 in range(TILES_PER_BANK):
+                        c = k * TILES_PER_BANK + c4
+                        column = past_key if c < r else later_key
+                        addends.append((c4, column[:, b, c * H + h : c * H + h + 1].to_broadcast([P, P])))
+                        if c == r:
+                            addends.append((c4, past_t[:]))
+                    for n, (c4, addend) in enumerate(addends):
+                        nc.tensor.matmul(
+                            out=banks[k][:, c4 * P : (c4 + 1) * P],
+                            lhsT=addend,
+                            rhs=ident_f[:],
+                            start=False,
+                            stop=(n == len(addends) - 1),
+                            is_transpose=True,
+                        )
+                tiles["s", i] = banks
+
+            def bank_maxima(i):
+                bank_max = rows.tile([P, BANKS_PER_ROW], F32, name="bank_max")
+                for k in range(BANKS_PER_ROW):
+                    nc.vector.tensor_reduce(out=bank_max[:, k : k + 1], in_=tiles["s", i][k][:], axis=AX.X, op=ALU.max)
+                tiles["max", i] = bank_max
+
+            def row_shift(i):
+                shift = rows.tile([P, 1], F32, name="shift")
+                bank_max = tiles["max", i]
+                nc.vector.tensor_scalar(
+                    out=shift[:],
+                    in0=bank_max[:, 0:1],
+                    scalar1=bank_max[:, 1:2],
+                    scalar2=-SCALE,
+                    op0=ALU.max,
+                    op1=ALU.mult,
+                )
+                tiles["shift", i] = shift
+
+            def exponentials(i):
+                if i % GROUP == 0:
+                    tiles["sums", i // GROUP] = groups.tile([P, GROUP, BANKS_PER_ROW], F32, name="row_sums")
+                e_sb = rows.tile([P, T], BF16, name="e_sb")
+                banks = tiles["s", i]
+                shift = tiles["shift", i]
+                for k in range(BANKS_PER_ROW):
+                    nc.scalar.activation(
+                        out=e_sb[:, k * BANK : (k + 1) * BANK],
+                        in_=banks[k][:],
+                        func=ACT.Exp,
+                        bias=shift[:],
+                        scale=SCALE,
+                        accum_out=tiles["sums", i // GROUP][:, i % GROUP, k : k + 1],
+                    )
+                tiles["e", i] = e_sb
+
+            def turn(i):
+                e_t = ps_r.tile([P, PASSES, 2, P], F32, name="e_t", tag="r")
+                e_words = tiles["e", i][:].bitcast(F32)
+                for g in range(PASSES):
+                    for u in range(2):
+                        w = 2 * g + u
+                        nc.tensor.transpose(out=e_t[:, g, u, :], in_=e_words[:, w * P : (w + 1) * P], identity=ident_f[:])
+                tiles["e_t", i] = e_t
+
+            def regroup(i):
+                e_grouped = rows.tile([P, PASSES * P * PACK], BF16, name="e_grouped", align_bytes=64)
+                nc.scalar.copy(
+                    out=e_grouped[:].bitcast(F32).rearrange("p (g q u) -> p g q u", g=PASSES, u=2),
+                    in_=tiles["e_t", i][:].rearrange("p g u q -> p g q u"),
+                )
+                tiles["grouped", i] = e_grouped
+
+            def quantise(i):
+                if i % GROUP == 0:
+                    tiles["codes", i // GROUP] = groups.tile(
+                        [P, GROUP * PASSES * P], U32, name="e_codes", align_bytes=64
+                    )
+                    tiles["scales", i // GROUP] = groups.tile(
+                        [P, GROUP * PASSES * P], U8, name="e_scales", align_bytes=64
+                    )
+                cols = slice((i % GROUP) * PASSES * P, (i % GROUP + 1) * PASSES * P)
+                nc.vector.quantize_mx(
+                    out=tiles["codes", i // GROUP][:, cols].bitcast(FP8X4),
+                    scales=tiles["scales", i // GROUP][:, cols],
+                    in_=tiles["grouped", i][:],
+                )
+
+            def sum_rows(m):
+                weight = groups.tile([P, GROUP], F32, name="weight")
+                nc.vector.tensor_reduce(out=weight[:], in_=tiles["sums", m][:], axis=AX.X, op=ALU.add)
+                tiles["weight", m] = weight
+
+            def invert_sums(m):
+                nc.vector.reciprocal(out=tiles["weight", m][:], in_=tiles["weight", m][:])
+
+            def weigh_rows(m):
+                b, h, r = where(m * GROUP)
+                nc.vector.tensor_tensor(
+                    out=tiles["weight", m][:], in0=tiles["weight", m][:], in1=row_on[:, b, r : r + GROUP, h], op=ALU.mult
+                )
+
+            def e_times_v(m):
+                b, h, r = where(m * GROUP)
+                o_ps = ps_r.tile([P, GROUP, DH], F32, name="o_ps", tag="r")
+                e_codes = tiles["codes", m]
+                e_scales = tiles["scales", m]
+                for n in range(GROUP):
+                    for g in range(PASSES):
+                        e_cols = slice((n * PASSES + g) * P, (n * PASSES + g + 1) * P)
+                        v_cols = slice((h * PASSES + g) * DH, (h * PASSES + g + 1) * DH)
+                        nc.tensor.matmul_mx(
+                            out=o_ps[:, n, :],
+                            lhsT=e_codes[:, e_cols].bitcast(FP8X4),
+                            lhsT_scale=e_scales[:, e_cols],
+                            rhs=v_codes[:, b, v_cols].bitcast(FP8X4),
+                            rhs_scale=v_scales[:, b, v_cols],
+                            start=(g == 0),
+                            stop=(g == PASSES - 1),
+                        )
+                tiles["o", m] = o_ps
+
+            def finish(m):
+                b, h, r = where(m * GROUP)
+                o_sb = groups.tile([P, GROUP, DH], F32, name="o_sb")
+                nc.vector.tensor_tensor(
+                    out=o_sb[:],
+                    in0=tiles["o", m][:],
+                    in1=tiles["weight", m][:].unsqueeze(2).to_broadcast([P, GROUP, DH]),
+                    op=ALU.mult,
+                )
+                nc.sync.dma_start(
+                    out=out[b].rearrange("(r p) d -> p r d", p=P)[:, r : r + GROUP, h * DH : (h + 1) * DH], in_=o_sb[:]
+                )
+
+            def tile_at(i):
+                return 0 <= i < ROW_TILES
+
+            def group_ends_at(i):
+                return tile_at(i) and i % GROUP == GROUP - 1
+
+            for step in range(ROW_TILES + LAG_FINISH + 1):
+                if tile_at(step - LAG_TURN):
+                    turn(step - LAG_TURN)
+                if group_ends_at(step - LAG_E_TIMES_V):
+                    e_times_v((step - LAG_E_TIMES_V) // GROUP)
+                if tile_at(step):
+                    scores(step)
+                if tile_at(step - LAG_EXP):
+                    exponentials(step - LAG_EXP)
+                if tile_at(step - LAG_TURN):
+                    regroup(step - LAG_TURN)
+                if tile_at(step - LAG_MAX):
+                    bank_maxima(step - LAG_MAX)
+                if tile_at(step - LAG_QUANTISE):
+                    quantise(step - LAG_QUANTISE)
+                if tile_at(step - LAG_MAX):
+                    row_shift(step - LAG_MAX)
+                if group_ends_at(step - LAG_SUM):
+                    sum_rows((step - LAG_SUM) // GROUP)
+                if group_ends_at(step - LAG_INVERT):
+                    invert_sums((step - LAG_INVERT) // GROUP)
+                if group_ends_at(step - LAG_WEIGH):
+                    weigh_rows((step - LAG_WEIGH) // GROUP)
+                if group_ends_at(step - LAG_FINISH):
+                    finish((step - LAG_FINISH) // GROUP)

@@ -38,9 +38,9 @@ LAG_TURN = 3
 LAG_QUANTISE = 4
 LAG_E_TIMES_V = 5
 LAG_SUM = 3
-LAG_INVERT = 4
-LAG_WEIGH = 5
-LAG_FINISH = 6
+LAG_WEIGH = 4
+LAG_FINISH = 5
+assert BANKS_PER_ROW == PASSES
 
 FLOPS = 2 * B * T * D * D + 2 * 2 * B * H * T * T * DH
 
@@ -220,42 +220,52 @@ def tile_multiheadattention_pa_t_kernel(tc, Q, K, x, Wv, mask, out):
             def where(i):
                 return i // (H * TILES), (i // TILES) % H, i % TILES
 
-            def scores(i):
+            def diagonal(i):
                 b, h, r = where(i)
-                banks = []
-                for k in range(BANKS_PER_ROW):
-                    s_ps = ps_s.tile([P, BANK], F32, name="s_ps", tag="s")
-                    banks.append(s_ps)
-                    nc.tensor.matmul(
-                        out=s_ps[:],
-                        lhsT=q_t[:, b, h, r * P : (r + 1) * P],
-                        rhs=k_t[:, b, h, k * BANK : (k + 1) * BANK],
-                        start=True,
-                        stop=False,
-                    )
-                for k in range(BANKS_PER_ROW):
-                    addends = []
-                    for c4 in range(TILES_PER_BANK):
-                        c = k * TILES_PER_BANK + c4
+                on_diagonal = rows.tile([P, P], F32, name="on_diagonal")
+                nc.vector.tensor_scalar(
+                    out=on_diagonal[:],
+                    in0=past_t[:],
+                    scalar1=later_key[:, b, r * H + h : r * H + h + 1],
+                    scalar2=None,
+                    op0=ALU.add,
+                )
+                tiles["diagonal", i] = on_diagonal
+
+            def products(i, k):
+                b, h, r = where(i)
+                s_ps = ps_s.tile([P, BANK], F32, name="s_ps", tag="s")
+                nc.tensor.matmul(
+                    out=s_ps[:],
+                    lhsT=q_t[:, b, h, r * P : (r + 1) * P],
+                    rhs=k_t[:, b, h, k * BANK : (k + 1) * BANK],
+                    start=True,
+                    stop=False,
+                )
+                tiles["s", i, k] = s_ps
+
+            def addends(i):
+                b, h, r = where(i)
+                for c in range(TILES):
+                    k, c4 = c // TILES_PER_BANK, c % TILES_PER_BANK
+                    if c == r:
+                        addend = tiles["diagonal", i][:]
+                    else:
                         column = past_key if c < r else later_key
-                        addends.append((c4, column[:, b, c * H + h : c * H + h + 1].to_broadcast([P, P])))
-                        if c == r:
-                            addends.append((c4, past_t[:]))
-                    for n, (c4, addend) in enumerate(addends):
-                        nc.tensor.matmul(
-                            out=banks[k][:, c4 * P : (c4 + 1) * P],
-                            lhsT=addend,
-                            rhs=ident_f[:],
-                            start=False,
-                            stop=(n == len(addends) - 1),
-                            is_transpose=True,
-                        )
-                tiles["s", i] = banks
+                        addend = column[:, b, c * H + h : c * H + h + 1].to_broadcast([P, P])
+                    nc.tensor.matmul(
+                        out=tiles["s", i, k][:, c4 * P : (c4 + 1) * P],
+                        lhsT=addend,
+                        rhs=ident_f[:],
+                        start=False,
+                        stop=(c4 == TILES_PER_BANK - 1),
+                        is_transpose=True,
+                    )
 
             def bank_maxima(i):
                 bank_max = rows.tile([P, BANKS_PER_ROW], F32, name="bank_max")
                 for k in range(BANKS_PER_ROW):
-                    nc.vector.tensor_reduce(out=bank_max[:, k : k + 1], in_=tiles["s", i][k][:], axis=AX.X, op=ALU.max)
+                    nc.vector.tensor_reduce(out=bank_max[:, k : k + 1], in_=tiles["s", i, k][:], axis=AX.X, op=ALU.max)
                 tiles["max", i] = bank_max
 
             def row_shift(i):
@@ -275,12 +285,11 @@ def tile_multiheadattention_pa_t_kernel(tc, Q, K, x, Wv, mask, out):
                 if i % GROUP == 0:
                     tiles["sums", i // GROUP] = groups.tile([P, GROUP, BANKS_PER_ROW], F32, name="row_sums")
                 e_sb = rows.tile([P, T], BF16, name="e_sb")
-                banks = tiles["s", i]
                 shift = tiles["shift", i]
                 for k in range(BANKS_PER_ROW):
                     nc.scalar.activation(
                         out=e_sb[:, k * BANK : (k + 1) * BANK],
-                        in_=banks[k][:],
+                        in_=tiles["s", i, k][:],
                         func=ACT.Exp,
                         bias=shift[:],
                         scale=SCALE,
@@ -288,14 +297,15 @@ def tile_multiheadattention_pa_t_kernel(tc, Q, K, x, Wv, mask, out):
                     )
                 tiles["e", i] = e_sb
 
-            def turn(i):
-                e_t = ps_r.tile([P, PASSES, 2, P], F32, name="e_t", tag="r")
+            def turn(i, g):
+                if g == 0:
+                    tiles["e_t", i] = ps_r.tile([P, PASSES, 2, P], F32, name="e_t", tag="r")
                 e_words = tiles["e", i][:].bitcast(F32)
-                for g in range(PASSES):
-                    for u in range(2):
-                        w = 2 * g + u
-                        nc.tensor.transpose(out=e_t[:, g, u, :], in_=e_words[:, w * P : (w + 1) * P], identity=ident_f[:])
-                tiles["e_t", i] = e_t
+                for u in range(2):
+                    w = 2 * g + u
+                    nc.tensor.transpose(
+                        out=tiles["e_t", i][:, g, u, :], in_=e_words[:, w * P : (w + 1) * P], identity=ident_f[:]
+                    )
 
             def regroup(i):
                 e_grouped = rows.tile([P, PASSES * P * PACK], BF16, name="e_grouped", align_bytes=64)
@@ -373,27 +383,33 @@ def tile_multiheadattention_pa_t_kernel(tc, Q, K, x, Wv, mask, out):
             def group_ends_at(i):
                 return tile_at(i) and i % GROUP == GROUP - 1
 
+            diagonal(0)
             for step in range(ROW_TILES + LAG_FINISH + 1):
-                if tile_at(step - LAG_TURN):
-                    turn(step - LAG_TURN)
                 if group_ends_at(step - LAG_E_TIMES_V):
                     e_times_v((step - LAG_E_TIMES_V) // GROUP)
+                for half in range(BANKS_PER_ROW):
+                    if tile_at(step):
+                        products(step, half)
+                    if tile_at(step - LAG_TURN):
+                        turn(step - LAG_TURN, half)
                 if tile_at(step):
-                    scores(step)
+                    addends(step)
                 if tile_at(step - LAG_EXP):
                     exponentials(step - LAG_EXP)
                 if tile_at(step - LAG_TURN):
                     regroup(step - LAG_TURN)
                 if tile_at(step - LAG_MAX):
                     bank_maxima(step - LAG_MAX)
+                if group_ends_at(step - LAG_SUM):
+                    sum_rows((step - LAG_SUM) // GROUP)
                 if tile_at(step - LAG_QUANTISE):
                     quantise(step - LAG_QUANTISE)
                 if tile_at(step - LAG_MAX):
                     row_shift(step - LAG_MAX)
+                if tile_at(step + 1):
+                    diagonal(step + 1)
                 if group_ends_at(step - LAG_SUM):
-                    sum_rows((step - LAG_SUM) // GROUP)
-                if group_ends_at(step - LAG_INVERT):
-                    invert_sums((step - LAG_INVERT) // GROUP)
+                    invert_sums((step - LAG_SUM) // GROUP)
                 if group_ends_at(step - LAG_WEIGH):
                     weigh_rows((step - LAG_WEIGH) // GROUP)
                 if group_ends_at(step - LAG_FINISH):

@@ -385,13 +385,19 @@ def tile_multiheadattention_pa_t_kernel(tc, Q, K, x, Wv, mask, out):
 
             diagonal(0)
             for step in range(ROW_TILES + LAG_FINISH + 1):
-                if group_ends_at(step - LAG_E_TIMES_V):
+                burst = group_ends_at(step - LAG_E_TIMES_V)
+                if tile_at(step):
+                    products(step, 0)
+                if burst:
                     e_times_v((step - LAG_E_TIMES_V) // GROUP)
-                for half in range(BANKS_PER_ROW):
-                    if tile_at(step):
-                        products(step, half)
-                    if tile_at(step - LAG_TURN):
-                        turn(step - LAG_TURN, half)
+                elif tile_at(step - LAG_TURN):
+                    turn(step - LAG_TURN, 0)
+                if tile_at(step):
+                    products(step, 1)
+                if burst and tile_at(step - LAG_TURN):
+                    turn(step - LAG_TURN, 0)
+                if tile_at(step - LAG_TURN):
+                    turn(step - LAG_TURN, 1)
                 if tile_at(step):
                     addends(step)
                 if tile_at(step - LAG_EXP):

@@ -223,12 +223,13 @@ def tile_multiheadattention_pa_t_kernel(tc, Q, K, x, Wv, mask, out):
             def diagonal(i):
                 b, h, r = where(i)
                 on_diagonal = rows.tile([P, P], F32, name="on_diagonal")
-                nc.vector.tensor_scalar(
+                nc.gpsimd.tensor_scalar(
                     out=on_diagonal[:],
                     in0=past_t[:],
                     scalar1=later_key[:, b, r * H + h : r * H + h + 1],
-                    scalar2=None,
+                    scalar2=1.0,
                     op0=ALU.add,
+                    op1=ALU.mult,
                 )
                 tiles["diagonal", i] = on_diagonal
 
@@ -244,10 +245,12 @@ def tile_multiheadattention_pa_t_kernel(tc, Q, K, x, Wv, mask, out):
                 )
                 tiles["s", i, k] = s_ps
 
-            def addends(i):
+            def addends(i, banks):
                 b, h, r = where(i)
                 for c in range(TILES):
                     k, c4 = c // TILES_PER_BANK, c % TILES_PER_BANK
+                    if k not in banks:
+                        continue
                     if c == r:
                         addend = tiles["diagonal", i][:]
                     else:
@@ -384,22 +387,22 @@ def tile_multiheadattention_pa_t_kernel(tc, Q, K, x, Wv, mask, out):
                 return tile_at(i) and i % GROUP == GROUP - 1
 
             diagonal(0)
+            diagonal(1)
             for step in range(ROW_TILES + LAG_FINISH + 1):
-                burst = group_ends_at(step - LAG_E_TIMES_V)
                 if tile_at(step):
                     products(step, 0)
-                if burst:
+                if group_ends_at(step - LAG_E_TIMES_V):
                     e_times_v((step - LAG_E_TIMES_V) // GROUP)
-                elif tile_at(step - LAG_TURN):
-                    turn(step - LAG_TURN, 0)
                 if tile_at(step):
                     products(step, 1)
-                if burst and tile_at(step - LAG_TURN):
+                if tile_at(step - LAG_TURN):
                     turn(step - LAG_TURN, 0)
                 if tile_at(step - LAG_TURN):
                     turn(step - LAG_TURN, 1)
                 if tile_at(step):
-                    addends(step)
+                    addends(step, (0,))
+                if tile_at(step):
+                    addends(step, (1,))
                 if tile_at(step - LAG_EXP):
                     exponentials(step - LAG_EXP)
                 if tile_at(step - LAG_TURN):
@@ -412,11 +415,11 @@ def tile_multiheadattention_pa_t_kernel(tc, Q, K, x, Wv, mask, out):
                     quantise(step - LAG_QUANTISE)
                 if tile_at(step - LAG_MAX):
                     row_shift(step - LAG_MAX)
-                if tile_at(step + 1):
-                    diagonal(step + 1)
                 if group_ends_at(step - LAG_SUM):
                     invert_sums((step - LAG_SUM) // GROUP)
                 if group_ends_at(step - LAG_WEIGH):
                     weigh_rows((step - LAG_WEIGH) // GROUP)
                 if group_ends_at(step - LAG_FINISH):
                     finish((step - LAG_FINISH) // GROUP)
+                if tile_at(step + 2):
+                    diagonal(step + 2)

@@ -26,6 +26,7 @@ BANKS_PER_ROW = T // BANK
 TILES_PER_BANK = BANK // P
 GROUP = BANK // DH
 ROW_TILES = B * H * TILES
+HEADS = B * H
 
 SCALE = 1.0 / math.sqrt(DH)
 ABSENT_KEY = (-(2.0**32) + 1.0) / SCALE
@@ -38,8 +39,10 @@ LAG_TURN = 3
 LAG_QUANTISE = 4
 LAG_E_TIMES_V = 5
 LAG_SUM = 3
+LAG_INVERT = 4
 LAG_WEIGH = 4
 LAG_FINISH = 5
+LEAD_DIAGONAL = 2
 assert BANKS_PER_ROW == PASSES
 
 FLOPS = 2 * B * T * D * D + 2 * 2 * B * H * T * T * DH
@@ -50,6 +53,42 @@ def tile_multiheadattention_pa_t_kernel(tc, Q, K, x, Wv, mask, out):
     with ExitStack() as ctx:
         const = ctx.enter_context(tc.tile_pool(name="const", bufs=1))
         keep = ctx.enter_context(tc.tile_pool(name="keep", bufs=1))
+        loads = ctx.enter_context(tc.tile_pool(name="loads", bufs=2))
+        work = ctx.enter_context(tc.tile_pool(name="work", bufs=2))
+        rows = ctx.enter_context(tc.tile_pool(name="rows", bufs=3))
+        groups = ctx.enter_context(tc.tile_pool(name="groups", bufs=3))
+        ps_s = ctx.enter_context(tc.psum_pool(name="ps_s", bufs=6))
+        ps_r = ctx.enter_context(tc.psum_pool(name="ps_r", bufs=2))
+        ctx.enter_context(tc.manual_schedule())
+
+        tiles = {}
+
+        def load_tokens(b, parts):
+            x_sb = loads.tile([P, TILES, D], BF16, name="x_sb")
+            step = TILES // 2 // parts
+            for n in range(parts):
+                nc.sync.dma_start(
+                    out=x_sb[:, 2 * n * step : 2 * (n + 1) * step, :].rearrange("p (a e) d -> p a (e d)", e=2),
+                    in_=x[b].rearrange("(a p e) d -> p a (e d)", p=P, e=2)[:, n * step : (n + 1) * step, :],
+                )
+            tiles["x", b] = x_sb
+
+        def load_rows(name, source, b):
+            row_tile = loads.tile([P, TILES, D], BF16, name=name + "_sb")
+            nc.sync.dma_start(out=row_tile[:], in_=source[b].rearrange("(c p) d -> p c d", p=P))
+            tiles[name, b] = row_tile
+
+        load_tokens(0, 2)
+        w_sb = const.tile([P, H, D], BF16, name="w_sb")
+        nc.sync.dma_start(out=w_sb[:], in_=Wv.rearrange("(h p) i -> p h i", p=P))
+        load_rows("k", K, 0)
+        mask_rows = const.tile([P, P], BF16, name="mask_rows")
+        nc.vector.memset(mask_rows[:], 0.0)
+        nc.sync.dma_start(out=mask_rows[0 : B * TILES, :], in_=mask.rearrange("b (r p) -> (b r) p", p=P))
+        load_rows("q", Q, 0)
+        load_rows("k", K, 1)
+        load_tokens(1, 1)
+        load_rows("q", Q, 1)
 
         ident_f = const.tile([P, P], F32, name="ident_f")
         make_identity(nc, ident_f[:])
@@ -67,6 +106,10 @@ def tile_multiheadattention_pa_t_kernel(tc, Q, K, x, Wv, mask, out):
             base=0,
             channel_multiplier=1,
         )
+        token_mask = const.tile([P, B, TILES], F32, name="token_mask")
+        w_grouped = const.tile([P, H * P * PACK], BF16, name="w_grouped", align_bytes=64)
+        w_codes = const.tile([P, H * P], U32, name="w_codes", align_bytes=64)
+        w_scales = const.tile([P, H * P], U8, name="w_scales", align_bytes=64)
 
         q_t = keep.tile([P, B, H, T], BF16, name="q_t")
         k_t = keep.tile([P, B, H, T], BF16, name="k_t")
@@ -76,350 +119,467 @@ def tile_multiheadattention_pa_t_kernel(tc, Q, K, x, Wv, mask, out):
         past_key = keep.tile([P, B, TILES * H], F32, name="past_key")
         row_on = keep.tile([P, B, TILES, H], F32, name="row_on")
 
-        with ExitStack() as phase:
-            loads = phase.enter_context(tc.tile_pool(name="loads", bufs=2))
-            work = phase.enter_context(tc.tile_pool(name="work", bufs=2))
-            once = phase.enter_context(tc.tile_pool(name="once", bufs=1))
-            ps_t = phase.enter_context(tc.psum_pool(name="ps_t", bufs=4))
-            ps_v = phase.enter_context(tc.psum_pool(name="ps_v", bufs=4))
+        def bank(shape, dtype, name, turn_bank):
+            if turn_bank:
+                return ps_r.tile(shape, dtype, name=name, tag="r")
+            return ps_s.tile(shape, dtype, name=name, tag="s")
 
-            def words_onto_partitions(sources, grouped_words):
-                turned = ps_t.tile([P, 2, 2, P], F32, name="turned", tag="t")
+        def words_unit(sources, grouped, codes, scales):
+            made = {}
+
+            def first(turn_bank):
+                turned = bank([P, 2, 2, P], F32, "turned", turn_bank)
                 for s in range(2):
                     words = sources[s].bitcast(F32)
                     for u in range(2):
                         nc.tensor.transpose(
                             out=turned[:, s, u, :], in_=words[:, u * P : (u + 1) * P], identity=ident_f[:]
                         )
-                nc.scalar.copy(
-                    out=grouped_words.rearrange("p (s r u) -> p s r u", s=2, u=2),
-                    in_=turned[:].rearrange("p s u r -> p s r u"),
+                made["turned"] = turned
+
+            def second(copy):
+                copy(
+                    out=grouped.bitcast(F32).rearrange("p (s r u) -> p s r u", s=2, u=2),
+                    in_=made["turned"][:].rearrange("p s u r -> p s r u"),
                 )
 
-            def largest_magnitude(tokens_sb, largest):
-                bits = once.tile([P, TILES * D // 2], I32, name="bits")
-                nc.vector.tensor_scalar(
-                    out=bits[:],
-                    in0=tokens_sb[:].bitcast(I32).rearrange("p c w -> p (c w)"),
-                    scalar1=MAGNITUDE_BITS,
-                    scalar2=None,
-                    op0=ALU.bitwise_and,
-                )
-                nc.vector.tensor_reduce(
-                    out=largest[:], in_=bits[:].rearrange("p (n w) -> p n w", w=DH // 2), axis=AX.X, op=ALU.max
-                )
+            def third():
+                nc.vector.quantize_mx(out=codes.bitcast(FP8X4), scales=scales, in_=grouped)
 
-            mask_rows = once.tile([P, P], BF16, name="mask_rows")
-            nc.vector.memset(mask_rows[:], 0.0)
-            nc.sync.dma_start(out=mask_rows[0 : B * TILES, :], in_=mask.rearrange("b (r p) -> (b r) p", p=P))
-            w_sb = once.tile([P, H, D], BF16, name="w_sb")
-            nc.sync.dma_start(out=w_sb[:], in_=Wv.rearrange("(h p) i -> p h i", p=P))
+            return first, second, third
 
-            mask_ps = ps_t.tile([P, P], BF16, name="mask_ps", tag="t")
-            nc.tensor.transpose(out=mask_ps[:], in_=mask_rows[:], identity=ident_b[:])
-            token_mask = once.tile([P, B, TILES], F32, name="token_mask")
-            nc.vector.tensor_copy(out=token_mask[:].rearrange("p b r -> p (b r)"), in_=mask_ps[:, 0 : B * TILES])
+        def weight_unit(pair):
+            cols = slice(2 * pair * P, 2 * (pair + 1) * P)
+            return words_unit(
+                [w_sb[:, 2 * pair, :], w_sb[:, 2 * pair + 1, :]],
+                w_grouped[:, 2 * pair * P * PACK : 2 * (pair + 1) * P * PACK],
+                w_codes[:, cols],
+                w_scales[:, cols],
+            )
 
-            w_grouped = once.tile([P, H * P * PACK], BF16, name="w_grouped", align_bytes=64)
-            for pair in range(H // 2):
-                words_onto_partitions(
-                    [w_sb[:, 2 * pair, :], w_sb[:, 2 * pair + 1, :]],
-                    w_grouped[:].bitcast(F32)[:, pair * BANK : (pair + 1) * BANK],
-                )
-            w_codes = once.tile([P, H * P], U32, name="w_codes", align_bytes=64)
-            w_scales = once.tile([P, H * P], U8, name="w_scales", align_bytes=64)
-            nc.vector.quantize_mx(out=w_codes[:].bitcast(FP8X4), scales=w_scales[:], in_=w_grouped[:])
+        def token_unit(b, pair):
+            if pair == 0:
+                tiles["xg", b] = work.tile([P, TILES * P * PACK], BF16, name="x_grouped", align_bytes=64)
+                tiles["xc", b] = work.tile([P, TILES * P], U32, name="x_codes", align_bytes=64)
+                tiles["xs", b] = work.tile([P, TILES * P], U8, name="x_scales", align_bytes=64)
+            x_sb = tiles["x", b]
+            cols = slice(2 * pair * P, 2 * (pair + 1) * P)
+            return words_unit(
+                [x_sb[:, 2 * pair, :], x_sb[:, 2 * pair + 1, :]],
+                tiles["xg", b][:, 2 * pair * P * PACK : 2 * (pair + 1) * P * PACK],
+                tiles["xc", b][:, cols],
+                tiles["xs", b][:, cols],
+            )
 
-            for b in range(B):
-                x_sb = loads.tile([P, TILES, D], BF16, name="x_sb")
-                nc.sync.dma_start(
-                    out=x_sb[:].rearrange("p (a e) d -> p a (e d)", e=2),
-                    in_=x[b].rearrange("(a p e) d -> p a (e d)", p=P, e=2),
-                )
-                k_sb = loads.tile([P, TILES, D], BF16, name="k_sb")
-                nc.sync.dma_start(out=k_sb[:], in_=K[b].rearrange("(c p) d -> p c d", p=P))
-                q_sb = loads.tile([P, TILES, D], BF16, name="q_sb")
-                nc.sync.dma_start(out=q_sb[:], in_=Q[b].rearrange("(c p) d -> p c d", p=P))
+        def head_unit(b, h, name, turned_sb):
+            made = {}
 
-                x_grouped = work.tile([P, TILES * P * PACK], BF16, name="x_grouped", align_bytes=64)
-                for pair in range(TILES // 2):
-                    words_onto_partitions(
-                        [x_sb[:, 2 * pair, :], x_sb[:, 2 * pair + 1, :]],
-                        x_grouped[:].bitcast(F32)[:, pair * BANK : (pair + 1) * BANK],
-                    )
-
-                k_abs = work.tile([P, TILES * H], F32, name="k_abs")
-                largest_magnitude(k_sb, k_abs)
-                nc.vector.tensor_scalar(
-                    out=later_key[:, b, :], in0=k_abs[:], scalar1=0.0, scalar2=ABSENT_KEY, op0=ALU.is_equal, op1=ALU.mult
-                )
-                x_codes = work.tile([P, TILES * P], U32, name="x_codes", align_bytes=64)
-                x_scales = work.tile([P, TILES * P], U8, name="x_scales", align_bytes=64)
-                nc.vector.quantize_mx(out=x_codes[:].bitcast(FP8X4), scales=x_scales[:], in_=x_grouped[:])
-                nc.vector.tensor_scalar_add(out=past_key[:, b, :], in0=later_key[:, b, :], scalar1=PAST_KEY)
-
-                q_abs = work.tile([P, TILES * H], F32, name="q_abs")
-                largest_magnitude(q_sb, q_abs)
-                nc.vector.tensor_scalar(
-                    out=row_on[:, b, :, :].rearrange("p c h -> p (c h)"),
-                    in0=q_abs[:],
-                    scalar1=0.0,
-                    scalar2=None,
-                    op0=ALU.is_gt,
-                )
-
-                for h in range(H):
-                    for source, turned_sb in ((k_sb, k_t), (q_sb, q_t)):
-                        turned_ps = ps_t.tile([P, T], BF16, name="turned_ps", tag="t")
-                        for c in range(TILES):
-                            nc.tensor.transpose(
-                                out=turned_ps[:, c * P : (c + 1) * P],
-                                in_=source[:, c, h * DH : (h + 1) * DH],
-                                identity=ident_b[:],
-                            )
-                        nc.scalar.copy(out=turned_sb[:, b, h, :], in_=turned_ps[:])
-
-                nc.vector.tensor_tensor(
-                    out=row_on[:, b, :, :],
-                    in0=row_on[:, b, :, :],
-                    in1=token_mask[:, b, :].unsqueeze(2).to_broadcast([P, TILES, H]),
-                    op=ALU.mult,
-                )
-
-                v_grouped = work.tile([P, H * PASSES * DH * PACK], BF16, name="v_grouped", align_bytes=64)
-                for h in range(H):
-                    for g in range(PASSES):
-                        v_ps = ps_v.tile([P, PACK, DH], F32, name="v_ps", tag="v")
-                        for t in range(PACK):
-                            s = PACK * g + t
-                            nc.tensor.matmul_mx(
-                                out=v_ps[:, t, :],
-                                lhsT=x_codes[:, s * P : (s + 1) * P].bitcast(FP8X4),
-                                lhsT_scale=x_scales[:, s * P : (s + 1) * P],
-                                rhs=w_codes[:, h * DH : (h + 1) * DH].bitcast(FP8X4),
-                                rhs_scale=w_scales[:, h * DH : (h + 1) * DH],
-                                start=True,
-                                stop=True,
-                            )
-                        piece = (h * PASSES + g) * DH * PACK
-                        nc.scalar.copy(
-                            out=v_grouped[:, piece : piece + DH * PACK].rearrange("p (d t) -> p d t", t=PACK),
-                            in_=v_ps[:].rearrange("p t d -> p d t"),
-                        )
-                nc.vector.quantize_mx(out=v_codes[:, b, :].bitcast(FP8X4), scales=v_scales[:, b, :], in_=v_grouped[:])
-
-        with ExitStack() as phase:
-            rows = phase.enter_context(tc.tile_pool(name="rows", bufs=3))
-            groups = phase.enter_context(tc.tile_pool(name="groups", bufs=3))
-            ps_s = phase.enter_context(tc.psum_pool(name="ps_s", bufs=6))
-            ps_r = phase.enter_context(tc.psum_pool(name="ps_r", bufs=2))
-            phase.enter_context(tc.manual_schedule())
-
-            tiles = {}
-
-            def where(i):
-                return i // (H * TILES), (i // TILES) % H, i % TILES
-
-            def diagonal(i):
-                b, h, r = where(i)
-                on_diagonal = rows.tile([P, P], F32, name="on_diagonal")
-                nc.gpsimd.tensor_scalar(
-                    out=on_diagonal[:],
-                    in0=past_t[:],
-                    scalar1=later_key[:, b, r * H + h : r * H + h + 1],
-                    scalar2=1.0,
-                    op0=ALU.add,
-                    op1=ALU.mult,
-                )
-                tiles["diagonal", i] = on_diagonal
-
-            def products(i, k):
-                b, h, r = where(i)
-                s_ps = ps_s.tile([P, BANK], F32, name="s_ps", tag="s")
-                nc.tensor.matmul(
-                    out=s_ps[:],
-                    lhsT=q_t[:, b, h, r * P : (r + 1) * P],
-                    rhs=k_t[:, b, h, k * BANK : (k + 1) * BANK],
-                    start=True,
-                    stop=False,
-                )
-                tiles["s", i, k] = s_ps
-
-            def addends(i, banks):
-                b, h, r = where(i)
+            def first(turn_bank):
+                turned = bank([P, T], BF16, "turned_head", turn_bank)
                 for c in range(TILES):
-                    k, c4 = c // TILES_PER_BANK, c % TILES_PER_BANK
-                    if k not in banks:
-                        continue
-                    if c == r:
-                        addend = tiles["diagonal", i][:]
-                    else:
-                        column = past_key if c < r else later_key
-                        addend = column[:, b, c * H + h : c * H + h + 1].to_broadcast([P, P])
-                    nc.tensor.matmul(
-                        out=tiles["s", i, k][:, c4 * P : (c4 + 1) * P],
-                        lhsT=addend,
-                        rhs=ident_f[:],
-                        start=False,
-                        stop=(c4 == TILES_PER_BANK - 1),
-                        is_transpose=True,
-                    )
-
-            def bank_maxima(i):
-                bank_max = rows.tile([P, BANKS_PER_ROW], F32, name="bank_max")
-                for k in range(BANKS_PER_ROW):
-                    nc.vector.tensor_reduce(out=bank_max[:, k : k + 1], in_=tiles["s", i, k][:], axis=AX.X, op=ALU.max)
-                tiles["max", i] = bank_max
-
-            def row_shift(i):
-                shift = rows.tile([P, 1], F32, name="shift")
-                bank_max = tiles["max", i]
-                nc.vector.tensor_scalar(
-                    out=shift[:],
-                    in0=bank_max[:, 0:1],
-                    scalar1=bank_max[:, 1:2],
-                    scalar2=-SCALE,
-                    op0=ALU.max,
-                    op1=ALU.mult,
-                )
-                tiles["shift", i] = shift
-
-            def exponentials(i):
-                if i % GROUP == 0:
-                    tiles["sums", i // GROUP] = groups.tile([P, GROUP, BANKS_PER_ROW], F32, name="row_sums")
-                e_sb = rows.tile([P, T], BF16, name="e_sb")
-                shift = tiles["shift", i]
-                for k in range(BANKS_PER_ROW):
-                    nc.scalar.activation(
-                        out=e_sb[:, k * BANK : (k + 1) * BANK],
-                        in_=tiles["s", i, k][:],
-                        func=ACT.Exp,
-                        bias=shift[:],
-                        scale=SCALE,
-                        accum_out=tiles["sums", i // GROUP][:, i % GROUP, k : k + 1],
-                    )
-                tiles["e", i] = e_sb
-
-            def turn(i, g):
-                if g == 0:
-                    tiles["e_t", i] = ps_r.tile([P, PASSES, 2, P], F32, name="e_t", tag="r")
-                e_words = tiles["e", i][:].bitcast(F32)
-                for u in range(2):
-                    w = 2 * g + u
                     nc.tensor.transpose(
-                        out=tiles["e_t", i][:, g, u, :], in_=e_words[:, w * P : (w + 1) * P], identity=ident_f[:]
+                        out=turned[:, c * P : (c + 1) * P],
+                        in_=tiles[name, b][:, c, h * DH : (h + 1) * DH],
+                        identity=ident_b[:],
                     )
+                made["turned"] = turned
 
-            def regroup(i):
-                e_grouped = rows.tile([P, PASSES * P * PACK], BF16, name="e_grouped", align_bytes=64)
-                nc.scalar.copy(
-                    out=e_grouped[:].bitcast(F32).rearrange("p (g q u) -> p g q u", g=PASSES, u=2),
-                    in_=tiles["e_t", i][:].rearrange("p g u q -> p g q u"),
+            def second(copy):
+                copy(out=turned_sb[:, b, h, :], in_=made["turned"][:])
+
+            return first, second, None
+
+        def value_unit(b, h, g):
+            made = {}
+
+            def first(turn_bank):
+                v_ps = bank([P, PACK, DH], F32, "v_ps", turn_bank)
+                for t in range(PACK):
+                    s = PACK * g + t
+                    nc.tensor.matmul_mx(
+                        out=v_ps[:, t, :],
+                        lhsT=tiles["xc", b][:, s * P : (s + 1) * P].bitcast(FP8X4),
+                        lhsT_scale=tiles["xs", b][:, s * P : (s + 1) * P],
+                        rhs=w_codes[:, h * DH : (h + 1) * DH].bitcast(FP8X4),
+                        rhs_scale=w_scales[:, h * DH : (h + 1) * DH],
+                        start=True,
+                        stop=True,
+                    )
+                made["v"] = v_ps
+
+            def second(copy):
+                if g == 0:
+                    tiles["vg", b, h] = work.tile([P, PASSES * DH * PACK], BF16, name="v_grouped", align_bytes=64)
+                copy(
+                    out=tiles["vg", b, h][:, g * DH * PACK : (g + 1) * DH * PACK].rearrange("p (d t) -> p d t", t=PACK),
+                    in_=made["v"][:].rearrange("p t d -> p d t"),
                 )
-                tiles["grouped", i] = e_grouped
 
-            def quantise(i):
-                if i % GROUP == 0:
-                    tiles["codes", i // GROUP] = groups.tile(
-                        [P, GROUP * PASSES * P], U32, name="e_codes", align_bytes=64
-                    )
-                    tiles["scales", i // GROUP] = groups.tile(
-                        [P, GROUP * PASSES * P], U8, name="e_scales", align_bytes=64
-                    )
-                cols = slice((i % GROUP) * PASSES * P, (i % GROUP + 1) * PASSES * P)
+            def third():
+                codes = slice(h * PASSES * DH, (h + 1) * PASSES * DH)
                 nc.vector.quantize_mx(
-                    out=tiles["codes", i // GROUP][:, cols].bitcast(FP8X4),
-                    scales=tiles["scales", i // GROUP][:, cols],
-                    in_=tiles["grouped", i][:],
+                    out=v_codes[:, b, codes].bitcast(FP8X4), scales=v_scales[:, b, codes], in_=tiles["vg", b, h][:]
                 )
 
-            def sum_rows(m):
-                weight = groups.tile([P, GROUP], F32, name="weight")
-                nc.vector.tensor_reduce(out=weight[:], in_=tiles["sums", m][:], axis=AX.X, op=ALU.add)
-                tiles["weight", m] = weight
+            return first, second, third if g == PASSES - 1 else None
 
-            def invert_sums(m):
-                nc.vector.reciprocal(out=tiles["weight", m][:], in_=tiles["weight", m][:])
+        def zero_test(b, name, half):
+            columns = TILES // 2 * H
+            made = {}
 
-            def weigh_rows(m):
-                b, h, r = where(m * GROUP)
+            def first_or():
+                words = tiles[name, b][:, half * TILES // 2 : (half + 1) * TILES // 2, :]
+                words = words.rearrange("p c d -> p (c d)").bitcast(I32).rearrange("p (n w) -> p n w", w=DH // 2)
+                made["32"] = work.tile([P, columns, DH // 4], I32, name="or_32")
                 nc.vector.tensor_tensor(
-                    out=tiles["weight", m][:], in0=tiles["weight", m][:], in1=row_on[:, b, r : r + GROUP, h], op=ALU.mult
+                    out=made["32"][:], in0=words[:, :, 0 : DH // 4], in1=words[:, :, DH // 4 :], op=ALU.bitwise_or
                 )
 
-            def e_times_v(m):
-                b, h, r = where(m * GROUP)
-                o_ps = ps_r.tile([P, GROUP, DH], F32, name="o_ps", tag="r")
-                e_codes = tiles["codes", m]
-                e_scales = tiles["scales", m]
-                for n in range(GROUP):
-                    for g in range(PASSES):
-                        e_cols = slice((n * PASSES + g) * P, (n * PASSES + g + 1) * P)
-                        v_cols = slice((h * PASSES + g) * DH, (h * PASSES + g + 1) * DH)
-                        nc.tensor.matmul_mx(
-                            out=o_ps[:, n, :],
-                            lhsT=e_codes[:, e_cols].bitcast(FP8X4),
-                            lhsT_scale=e_scales[:, e_cols],
-                            rhs=v_codes[:, b, v_cols].bitcast(FP8X4),
-                            rhs_scale=v_scales[:, b, v_cols],
-                            start=(g == 0),
-                            stop=(g == PASSES - 1),
-                        )
-                tiles["o", m] = o_ps
-
-            def finish(m):
-                b, h, r = where(m * GROUP)
-                o_sb = groups.tile([P, GROUP, DH], F32, name="o_sb")
+            def second_or():
+                words = made["32"]
+                made["16"] = work.tile([P, columns, DH // 8], I32, name="or_16")
                 nc.vector.tensor_tensor(
-                    out=o_sb[:],
-                    in0=tiles["o", m][:],
-                    in1=tiles["weight", m][:].unsqueeze(2).to_broadcast([P, GROUP, DH]),
-                    op=ALU.mult,
-                )
-                nc.sync.dma_start(
-                    out=out[b].rearrange("(r p) d -> p r d", p=P)[:, r : r + GROUP, h * DH : (h + 1) * DH], in_=o_sb[:]
+                    out=made["16"][:], in0=words[:, :, 0 : DH // 8], in1=words[:, :, DH // 8 :], op=ALU.bitwise_or
                 )
 
-            def tile_at(i):
-                return 0 <= i < ROW_TILES
+            def drop_signs():
+                made["bits"] = work.tile([P, columns, DH // 8], I32, name="bits")
+                nc.vector.tensor_scalar(
+                    out=made["bits"][:], in0=made["16"][:], scalar1=MAGNITUDE_BITS, scalar2=None, op0=ALU.bitwise_and
+                )
 
-            def group_ends_at(i):
-                return tile_at(i) and i % GROUP == GROUP - 1
+            def largest():
+                if half == 0:
+                    tiles["largest", b, name] = work.tile([P, TILES * H], F32, name="largest_" + name)
+                nc.vector.tensor_reduce(
+                    out=tiles["largest", b, name][:, half * columns : (half + 1) * columns],
+                    in_=made["bits"][:],
+                    axis=AX.X,
+                    op=ALU.max,
+                )
 
-            diagonal(0)
-            diagonal(1)
-            for step in range(ROW_TILES + LAG_FINISH + 1):
-                if tile_at(step):
-                    products(step, 0)
-                if group_ends_at(step - LAG_E_TIMES_V):
-                    e_times_v((step - LAG_E_TIMES_V) // GROUP)
-                if tile_at(step):
-                    products(step, 1)
+            return [first_or, second_or, drop_signs, largest]
+
+        def absent_keys(b):
+            nc.vector.tensor_scalar(
+                out=later_key[:, b, :],
+                in0=tiles["largest", b, "k"][:],
+                scalar1=0.0,
+                scalar2=ABSENT_KEY,
+                op0=ALU.is_equal,
+                op1=ALU.mult,
+            )
+
+        def past_keys(b):
+            nc.vector.tensor_scalar_add(out=past_key[:, b, :], in0=later_key[:, b, :], scalar1=PAST_KEY)
+
+        def row_weights(b):
+            nc.vector.scalar_tensor_tensor(
+                out=row_on[:, b, :, :],
+                in0=tiles["largest", b, "q"][:].rearrange("p (c h) -> p c h", h=H),
+                scalar=0.0,
+                in1=token_mask[:, b, :].unsqueeze(2).to_broadcast([P, TILES, H]),
+                op0=ALU.is_gt,
+                op1=ALU.mult,
+            )
+
+        def where(i):
+            return i // (H * TILES), (i // TILES) % H, i % TILES
+
+        def diagonal(i):
+            b, h, r = where(i)
+            on_diagonal = rows.tile([P, P], F32, name="on_diagonal")
+            nc.gpsimd.tensor_scalar(
+                out=on_diagonal[:],
+                in0=past_t[:],
+                scalar1=later_key[:, b, r * H + h : r * H + h + 1],
+                scalar2=1.0,
+                op0=ALU.add,
+                op1=ALU.mult,
+            )
+            tiles["diagonal", i] = on_diagonal
+
+        def products(i, k):
+            b, h, r = where(i)
+            s_ps = ps_s.tile([P, BANK], F32, name="s_ps", tag="s")
+            nc.tensor.matmul(
+                out=s_ps[:],
+                lhsT=q_t[:, b, h, r * P : (r + 1) * P],
+                rhs=k_t[:, b, h, k * BANK : (k + 1) * BANK],
+                start=True,
+                stop=False,
+            )
+            tiles["s", i, k] = s_ps
+
+        def addends(i):
+            b, h, r = where(i)
+            for c in range(TILES):
+                k, c4 = c // TILES_PER_BANK, c % TILES_PER_BANK
+                if c == r:
+                    addend = tiles["diagonal", i][:]
+                else:
+                    column = past_key if c < r else later_key
+                    addend = column[:, b, c * H + h : c * H + h + 1].to_broadcast([P, P])
+                nc.tensor.matmul(
+                    out=tiles["s", i, k][:, c4 * P : (c4 + 1) * P],
+                    lhsT=addend,
+                    rhs=ident_f[:],
+                    start=False,
+                    stop=(c4 == TILES_PER_BANK - 1),
+                    is_transpose=True,
+                )
+
+        def bank_maxima(i):
+            bank_max = rows.tile([P, BANKS_PER_ROW], F32, name="bank_max")
+            for k in range(BANKS_PER_ROW):
+                nc.vector.tensor_reduce(out=bank_max[:, k : k + 1], in_=tiles["s", i, k][:], axis=AX.X, op=ALU.max)
+            tiles["max", i] = bank_max
+
+        def row_shift(i):
+            shift = rows.tile([P, 1], F32, name="shift")
+            bank_max = tiles["max", i]
+            nc.vector.tensor_scalar(
+                out=shift[:],
+                in0=bank_max[:, 0:1],
+                scalar1=bank_max[:, 1:2],
+                scalar2=-SCALE,
+                op0=ALU.max,
+                op1=ALU.mult,
+            )
+            tiles["shift", i] = shift
+
+        def exponentials(i):
+            if i % GROUP == 0:
+                tiles["sums", i // GROUP] = groups.tile([P, GROUP, BANKS_PER_ROW], F32, name="row_sums")
+            e_sb = rows.tile([P, T], BF16, name="e_sb")
+            shift = tiles["shift", i]
+            for k in range(BANKS_PER_ROW):
+                nc.scalar.activation(
+                    out=e_sb[:, k * BANK : (k + 1) * BANK],
+                    in_=tiles["s", i, k][:],
+                    func=ACT.Exp,
+                    bias=shift[:],
+                    scale=SCALE,
+                    accum_out=tiles["sums", i // GROUP][:, i % GROUP, k : k + 1],
+                )
+            tiles["e", i] = e_sb
+
+        def turn(i, g):
+            if g == 0:
+                tiles["e_t", i] = ps_r.tile([P, PASSES, 2, P], F32, name="e_t", tag="r")
+            e_words = tiles["e", i][:].bitcast(F32)
+            for u in range(2):
+                w = 2 * g + u
+                nc.tensor.transpose(
+                    out=tiles["e_t", i][:, g, u, :], in_=e_words[:, w * P : (w + 1) * P], identity=ident_f[:]
+                )
+
+        def regroup(i):
+            e_grouped = rows.tile([P, PASSES * P * PACK], BF16, name="e_grouped", align_bytes=64)
+            copy = nc.vector.tensor_copy if on_vector(i) else nc.scalar.copy
+            copy(
+                out=e_grouped[:].bitcast(F32).rearrange("p (g q u) -> p g q u", g=PASSES, u=2),
+                in_=tiles["e_t", i][:].rearrange("p g u q -> p g q u"),
+            )
+            tiles["grouped", i] = e_grouped
+
+        def quantise(i):
+            if i % GROUP == 0:
+                tiles["codes", i // GROUP] = groups.tile(
+                    [P, GROUP * PASSES * P], U32, name="e_codes", align_bytes=64
+                )
+                tiles["scales", i // GROUP] = groups.tile(
+                    [P, GROUP * PASSES * P], U8, name="e_scales", align_bytes=64
+                )
+            cols = slice((i % GROUP) * PASSES * P, (i % GROUP + 1) * PASSES * P)
+            nc.vector.quantize_mx(
+                out=tiles["codes", i // GROUP][:, cols].bitcast(FP8X4),
+                scales=tiles["scales", i // GROUP][:, cols],
+                in_=tiles["grouped", i][:],
+            )
+
+        def sum_rows(m):
+            weight = groups.tile([P, GROUP], F32, name="weight")
+            sums = tiles["sums", m]
+            nc.gpsimd.tensor_tensor(out=weight[:], in0=sums[:, :, 0], in1=sums[:, :, 1], op=ALU.add)
+            tiles["weight", m] = weight
+
+        def invert_sums(m):
+            nc.vector.reciprocal(out=tiles["weight", m][:], in_=tiles["weight", m][:])
+
+        def weigh_rows(m):
+            b, h, r = where(m * GROUP)
+            nc.gpsimd.tensor_tensor(
+                out=tiles["weight", m][:], in0=tiles["weight", m][:], in1=row_on[:, b, r : r + GROUP, h], op=ALU.mult
+            )
+
+        def e_times_v(m):
+            b, h, r = where(m * GROUP)
+            o_ps = ps_r.tile([P, GROUP, DH], F32, name="o_ps", tag="r")
+            e_codes = tiles["codes", m]
+            e_scales = tiles["scales", m]
+            for n in range(GROUP):
+                for g in range(PASSES):
+                    e_cols = slice((n * PASSES + g) * P, (n * PASSES + g + 1) * P)
+                    v_cols = slice((h * PASSES + g) * DH, (h * PASSES + g + 1) * DH)
+                    nc.tensor.matmul_mx(
+                        out=o_ps[:, n, :],
+                        lhsT=e_codes[:, e_cols].bitcast(FP8X4),
+                        lhsT_scale=e_scales[:, e_cols],
+                        rhs=v_codes[:, b, v_cols].bitcast(FP8X4),
+                        rhs_scale=v_scales[:, b, v_cols],
+                        start=(g == 0),
+                        stop=(g == PASSES - 1),
+                    )
+            tiles["o", m] = o_ps
+
+        def finish(m):
+            b, h, r = where(m * GROUP)
+            o_sb = groups.tile([P, GROUP, DH], F32, name="o_sb")
+            nc.vector.tensor_tensor(
+                out=o_sb[:],
+                in0=tiles["o", m][:],
+                in1=tiles["weight", m][:].unsqueeze(2).to_broadcast([P, GROUP, DH]),
+                op=ALU.mult,
+            )
+            nc.sync.dma_start(
+                out=out[b].rearrange("(r p) d -> p r d", p=P)[:, r : r + GROUP, h * DH : (h + 1) * DH], in_=o_sb[:]
+            )
+
+        def tile_at(i):
+            return 0 <= i < ROW_TILES
+
+        def group_ends_at(i):
+            return tile_at(i) and i % GROUP == GROUP - 1
+        unit_count = [0]
+
+        def fill(unit):
+            unit[0](unit_count[0] % 4 == 3)
+            unit_count[0] = unit_count[0] + 1
+
+        def empty(unit, on_vector):
+            unit[1](nc.vector.tensor_copy if on_vector else nc.scalar.copy)
+
+        tokens = [token_unit(0, pair) for pair in range(TILES // 2)]
+        weights = [weight_unit(pair) for pair in range(H // 2)]
+        head_keys = [head_unit(0, h, "k", k_t) for h in range(H)]
+        for unit in tokens + weights:
+            fill(unit)
+        for n in range(TILES // 2):
+            empty(tokens[n], n % 2)
+        for unit in tokens:
+            unit[2]()
+        for n in range(H // 2):
+            empty(weights[n], n % 2)
+        for unit in head_keys:
+            fill(unit)
+            empty(unit, False)
+        for unit in weights:
+            unit[2]()
+        for steps in zip(zero_test(0, "k", 0), zero_test(0, "k", 1)):
+            for test_step in steps:
+                test_step()
+        mask_ps = ps_r.tile([P, P], BF16, name="mask_ps", tag="r")
+        nc.tensor.transpose(out=mask_ps[:], in_=mask_rows[:], identity=ident_b[:])
+        nc.vector.tensor_copy(out=token_mask[:].rearrange("p b r -> p (b r)"), in_=mask_ps[:, 0 : B * TILES])
+        absent_keys(0)
+
+        quantisers = []
+        chores = [lambda: past_keys(0)]
+        late = []
+        late_tests = []
+        for b in range(B):
+            for h in range(H):
+                if h == 0 and 1 <= b < B - 1:
+                    load_rows("k", K, b + 1)
+                    load_tokens(b + 1, 1)
+                    load_rows("q", Q, b + 1)
+                queries = [head_unit(b, h, "q", q_t)]
+                values = [value_unit(b, h, 0), value_unit(b, h, 1)]
+                following = [head_unit(b + 1, h, "k", k_t), token_unit(b + 1, h)] if b + 1 < B else []
+                group = queries + values + following if b == 0 else queries + following + values
+                if h % 2 == 0:
+                    test = zero_test(b, "q", h // 2)
+                elif b + 1 < B:
+                    test = zero_test(b + 1, "k", h // 2)
+                else:
+                    test = []
+                if b == B - 1 and h >= 3:
+                    late = late + group
+                    late_tests = late_tests + test
+                    continue
+                for n in range(3):
+                    if n < len(test):
+                        test[n]()
+                    if n < len(quantisers):
+                        quantisers[n]()
+                quantisers = []
+                for unit in group:
+                    fill(unit)
+                    empty(unit, following and unit is following[-1] and h % 2 == 1)
+                    if unit[2]:
+                        quantisers = quantisers + [unit[2]]
+                if chores:
+                    chores[0]()
+                    chores = chores[1:]
+                if test:
+                    test[3]()
+                if h == 2:
+                    chores = chores + [lambda batch=b: row_weights(batch)]
+                if h == 3 and b + 1 < B:
+                    chores = chores + [lambda batch=b + 1: absent_keys(batch), lambda batch=b + 1: past_keys(batch)]
+        for quantiser in quantisers:
+            quantiser()
+        for chore in chores:
+            chore()
+        def on_vector(i):
+            return i % 8 == 2
+
+        for i in range(LEAD_DIAGONAL):
+            diagonal(i)
+        for step in range(ROW_TILES + LAG_FINISH + 1):
+            if tile_at(step):
+                products(step, 0)
+            if group_ends_at(step - LAG_E_TIMES_V):
+                e_times_v((step - LAG_E_TIMES_V) // GROUP)
+            if tile_at(step):
+                products(step, 1)
+            for k in range(PASSES):
                 if tile_at(step - LAG_TURN):
-                    turn(step - LAG_TURN, 0)
-                if tile_at(step - LAG_TURN):
-                    turn(step - LAG_TURN, 1)
-                if tile_at(step):
-                    addends(step, (0,))
-                if tile_at(step):
-                    addends(step, (1,))
-                if tile_at(step - LAG_EXP):
-                    exponentials(step - LAG_EXP)
-                if tile_at(step - LAG_TURN):
-                    regroup(step - LAG_TURN)
-                if tile_at(step - LAG_MAX):
-                    bank_maxima(step - LAG_MAX)
-                if group_ends_at(step - LAG_SUM):
-                    sum_rows((step - LAG_SUM) // GROUP)
-                if tile_at(step - LAG_QUANTISE):
-                    quantise(step - LAG_QUANTISE)
-                if tile_at(step - LAG_MAX):
-                    row_shift(step - LAG_MAX)
-                if group_ends_at(step - LAG_SUM):
-                    invert_sums((step - LAG_SUM) // GROUP)
-                if group_ends_at(step - LAG_WEIGH):
-                    weigh_rows((step - LAG_WEIGH) // GROUP)
-                if group_ends_at(step - LAG_FINISH):
-                    finish((step - LAG_FINISH) // GROUP)
-                if tile_at(step + 2):
-                    diagonal(step + 2)
+                    turn(step - LAG_TURN, k)
+            if tile_at(step):
+                addends(step)
+            if step == 1:
+                for n in range(len(late)):
+                    late[n][0](n // 2 % 2 == 0)
+                    empty(late[n], False)
+            if tile_at(step - LAG_EXP):
+                exponentials(step - LAG_EXP)
+            if tile_at(step - LAG_TURN) and not on_vector(step - LAG_TURN):
+                regroup(step - LAG_TURN)
+            if group_ends_at(step - LAG_INVERT):
+                invert_sums((step - LAG_INVERT) // GROUP)
+            if group_ends_at(step - LAG_WEIGH):
+                weigh_rows((step - LAG_WEIGH) // GROUP)
+            if tile_at(step - LAG_MAX):
+                bank_maxima(step - LAG_MAX)
+            if group_ends_at(step - LAG_FINISH):
+                finish((step - LAG_FINISH) // GROUP)
+            if group_ends_at(step - LAG_SUM):
+                sum_rows((step - LAG_SUM) // GROUP)
+            if tile_at(step - LAG_QUANTISE):
+                quantise(step - LAG_QUANTISE)
+            if tile_at(step - LAG_MAX):
+                row_shift(step - LAG_MAX)
+            if tile_at(step - LAG_TURN) and on_vector(step - LAG_TURN):
+                regroup(step - LAG_TURN)
+            if step == 1 + 1:
+                for unit in late:
+                    if unit[2]:
+                        unit[2]()
+            if 0 <= step - 1 - 2 < len(late_tests):
+                late_tests[step - 1 - 2]()
+            if late_tests and step == 1 + 2 + len(late_tests):
+                row_weights(B - 1)
+            if tile_at(step + LEAD_DIAGONAL):
+                diagonal(step + LEAD_DIAGONAL)

@@ -78,7 +78,7 @@ def tile_multiheadattention_pa_t_kernel(tc, Q, K, x, Wv, mask, out):
             nc.sync.dma_start(out=row_tile[:], in_=source[b].rearrange("(c p) d -> p c d", p=P))
             tiles[name, b] = row_tile
 
-        load_tokens(0, 2)
+        load_tokens(0, 4)
         w_sb = const.tile([P, H, D], BF16, name="w_sb")
         nc.sync.dma_start(out=w_sb[:], in_=Wv.rearrange("(h p) i -> p h i", p=P))
         load_rows("k", K, 0)
@@ -261,7 +261,7 @@ def tile_multiheadattention_pa_t_kernel(tc, Q, K, x, Wv, mask, out):
             return [first_or, second_or, drop_signs, largest]
 
         def absent_keys(b):
-            nc.vector.tensor_scalar(
+            nc.gpsimd.tensor_scalar(
                 out=later_key[:, b, :],
                 in0=tiles["largest", b, "k"][:],
                 scalar1=0.0,
@@ -271,7 +271,14 @@ def tile_multiheadattention_pa_t_kernel(tc, Q, K, x, Wv, mask, out):
             )
 
         def past_keys(b):
-            nc.vector.tensor_scalar_add(out=past_key[:, b, :], in0=later_key[:, b, :], scalar1=PAST_KEY)
+            nc.gpsimd.tensor_scalar(
+                out=past_key[:, b, :],
+                in0=later_key[:, b, :],
+                scalar1=PAST_KEY,
+                scalar2=1.0,
+                op0=ALU.add,
+                op1=ALU.mult,
+            )
 
         def row_weights(b):
             nc.vector.scalar_tensor_tensor(
@@ -374,16 +381,15 @@ def tile_multiheadattention_pa_t_kernel(tc, Q, K, x, Wv, mask, out):
                     out=tiles["e_t", i][:, g, u, :], in_=e_words[:, w * P : (w + 1) * P], identity=ident_f[:]
                 )
 
-        def regroup(i):
-            e_grouped = rows.tile([P, PASSES * P * PACK], BF16, name="e_grouped", align_bytes=64)
-            copy = nc.vector.tensor_copy if on_vector(i) else nc.scalar.copy
+        def regroup(i, copy, passes=slice(0, PASSES)):
+            if ("grouped", i) not in tiles:
+                tiles["grouped", i] = rows.tile([P, PASSES * P * PACK], BF16, name="e_grouped", align_bytes=64)
             copy(
-                out=e_grouped[:].bitcast(F32).rearrange("p (g q u) -> p g q u", g=PASSES, u=2),
-                in_=tiles["e_t", i][:].rearrange("p g u q -> p g q u"),
+                out=tiles["grouped", i][:].bitcast(F32).rearrange("p (g q u) -> p g q u", g=PASSES, u=2)[:, passes],
+                in_=tiles["e_t", i][:].rearrange("p g u q -> p g q u")[:, passes],
             )
-            tiles["grouped", i] = e_grouped
 
-        def quantise(i):
+        def quantise(i, passes=range(PASSES)):
             if i % GROUP == 0:
                 tiles["codes", i // GROUP] = groups.tile(
                     [P, GROUP * PASSES * P], U32, name="e_codes", align_bytes=64
@@ -391,39 +397,41 @@ def tile_multiheadattention_pa_t_kernel(tc, Q, K, x, Wv, mask, out):
                 tiles["scales", i // GROUP] = groups.tile(
                     [P, GROUP * PASSES * P], U8, name="e_scales", align_bytes=64
                 )
-            cols = slice((i % GROUP) * PASSES * P, (i % GROUP + 1) * PASSES * P)
+            first, last = passes[0], passes[-1] + 1
+            cols = slice((i % GROUP * PASSES + first) * P, (i % GROUP * PASSES + last) * P)
             nc.vector.quantize_mx(
                 out=tiles["codes", i // GROUP][:, cols].bitcast(FP8X4),
                 scales=tiles["scales", i // GROUP][:, cols],
-                in_=tiles["grouped", i][:],
+                in_=tiles["grouped", i][:, first * P * PACK : last * P * PACK],
             )
 
-        def sum_rows(m):
+        def sum_rows(m, engine):
             weight = groups.tile([P, GROUP], F32, name="weight")
             sums = tiles["sums", m]
-            nc.gpsimd.tensor_tensor(out=weight[:], in0=sums[:, :, 0], in1=sums[:, :, 1], op=ALU.add)
+            engine.tensor_tensor(out=weight[:], in0=sums[:, :, 0], in1=sums[:, :, 1], op=ALU.add)
             tiles["weight", m] = weight
 
         def invert_sums(m):
             nc.vector.reciprocal(out=tiles["weight", m][:], in_=tiles["weight", m][:])
 
-        def weigh_rows(m):
+        def weigh_rows(m, engine):
             b, h, r = where(m * GROUP)
-            nc.gpsimd.tensor_tensor(
+            engine.tensor_tensor(
                 out=tiles["weight", m][:], in0=tiles["weight", m][:], in1=row_on[:, b, r : r + GROUP, h], op=ALU.mult
             )
 
-        def e_times_v(m):
+        def e_times_v(m, members=range(GROUP)):
             b, h, r = where(m * GROUP)
-            o_ps = ps_r.tile([P, GROUP, DH], F32, name="o_ps", tag="r")
+            o_ps = bank([P, len(members), DH], F32, "o_ps", members[0] == 0)
+            tiles["o", m, members[0]] = o_ps
             e_codes = tiles["codes", m]
             e_scales = tiles["scales", m]
-            for n in range(GROUP):
+            for n in members:
                 for g in range(PASSES):
                     e_cols = slice((n * PASSES + g) * P, (n * PASSES + g + 1) * P)
                     v_cols = slice((h * PASSES + g) * DH, (h * PASSES + g + 1) * DH)
                     nc.tensor.matmul_mx(
-                        out=o_ps[:, n, :],
+                        out=o_ps[:, n - members[0], :],
                         lhsT=e_codes[:, e_cols].bitcast(FP8X4),
                         lhsT_scale=e_scales[:, e_cols],
                         rhs=v_codes[:, b, v_cols].bitcast(FP8X4),
@@ -431,19 +439,19 @@ def tile_multiheadattention_pa_t_kernel(tc, Q, K, x, Wv, mask, out):
                         start=(g == 0),
                         stop=(g == PASSES - 1),
                     )
-            tiles["o", m] = o_ps
 
-        def finish(m):
+        def finish(m, first=0, last=GROUP):
             b, h, r = where(m * GROUP)
             o_sb = groups.tile([P, GROUP, DH], F32, name="o_sb")
             nc.vector.tensor_tensor(
-                out=o_sb[:],
-                in0=tiles["o", m][:],
-                in1=tiles["weight", m][:].unsqueeze(2).to_broadcast([P, GROUP, DH]),
+                out=o_sb[:, first:last, :],
+                in0=tiles["o", m, first][:],
+                in1=tiles["weight", m][:, first:last].unsqueeze(2).to_broadcast([P, last - first, DH]),
                 op=ALU.mult,
             )
             nc.sync.dma_start(
-                out=out[b].rearrange("(r p) d -> p r d", p=P)[:, r : r + GROUP, h * DH : (h + 1) * DH], in_=o_sb[:]
+                out=out[b].rearrange("(r p) d -> p r d", p=P)[:, r + first : r + last, h * DH : (h + 1) * DH],
+                in_=o_sb[:, first:last, :],
             )
 
         def tile_at(i):
@@ -451,6 +459,9 @@ def tile_multiheadattention_pa_t_kernel(tc, Q, K, x, Wv, mask, out):
 
         def group_ends_at(i):
             return tile_at(i) and i % GROUP == GROUP - 1
+        def whole_group_ends_at(i):
+            return group_ends_at(i) and i != ROW_TILES - 1
+
         unit_count = [0]
 
         def fill(unit):
@@ -497,7 +508,7 @@ def tile_multiheadattention_pa_t_kernel(tc, Q, K, x, Wv, mask, out):
                 queries = [head_unit(b, h, "q", q_t)]
                 values = [value_unit(b, h, 0), value_unit(b, h, 1)]
                 following = [head_unit(b + 1, h, "k", k_t), token_unit(b + 1, h)] if b + 1 < B else []
-                group = queries + values + following if b == 0 else queries + following + values
+                group = queries + following + values
                 if h % 2 == 0:
                     test = zero_test(b, "q", h // 2)
                 elif b + 1 < B:
@@ -533,14 +544,14 @@ def tile_multiheadattention_pa_t_kernel(tc, Q, K, x, Wv, mask, out):
         for chore in chores:
             chore()
         def on_vector(i):
-            return i % 8 == 2
+            return i % 8 == 2 or i == ROW_TILES - 2
 
         for i in range(LEAD_DIAGONAL):
             diagonal(i)
-        for step in range(ROW_TILES + LAG_FINISH + 1):
+        for step in range(ROW_TILES + LAG_EXP):
             if tile_at(step):
                 products(step, 0)
-            if group_ends_at(step - LAG_E_TIMES_V):
+            if whole_group_ends_at(step - LAG_E_TIMES_V):
                 e_times_v((step - LAG_E_TIMES_V) // GROUP)
             if tile_at(step):
                 products(step, 1)
@@ -549,37 +560,53 @@ def tile_multiheadattention_pa_t_kernel(tc, Q, K, x, Wv, mask, out):
                     turn(step - LAG_TURN, k)
             if tile_at(step):
                 addends(step)
-            if step == 1:
-                for n in range(len(late)):
-                    late[n][0](n // 2 % 2 == 0)
+            for n in range(len(late)):
+                if step == (0, 1, 1)[n]:
+                    late[n][0](True)
                     empty(late[n], False)
             if tile_at(step - LAG_EXP):
                 exponentials(step - LAG_EXP)
             if tile_at(step - LAG_TURN) and not on_vector(step - LAG_TURN):
-                regroup(step - LAG_TURN)
-            if group_ends_at(step - LAG_INVERT):
+                regroup(step - LAG_TURN, nc.scalar.copy)
+            if whole_group_ends_at(step - LAG_INVERT):
                 invert_sums((step - LAG_INVERT) // GROUP)
-            if group_ends_at(step - LAG_WEIGH):
-                weigh_rows((step - LAG_WEIGH) // GROUP)
+            if whole_group_ends_at(step - LAG_WEIGH):
+                weigh_rows((step - LAG_WEIGH) // GROUP, nc.gpsimd)
             if tile_at(step - LAG_MAX):
                 bank_maxima(step - LAG_MAX)
-            if group_ends_at(step - LAG_FINISH):
+            if whole_group_ends_at(step - LAG_FINISH):
                 finish((step - LAG_FINISH) // GROUP)
-            if group_ends_at(step - LAG_SUM):
-                sum_rows((step - LAG_SUM) // GROUP)
+            if whole_group_ends_at(step - LAG_SUM):
+                sum_rows((step - LAG_SUM) // GROUP, nc.gpsimd)
             if tile_at(step - LAG_QUANTISE):
                 quantise(step - LAG_QUANTISE)
             if tile_at(step - LAG_MAX):
                 row_shift(step - LAG_MAX)
             if tile_at(step - LAG_TURN) and on_vector(step - LAG_TURN):
-                regroup(step - LAG_TURN)
-            if step == 1 + 1:
+                regroup(step - LAG_TURN, nc.vector.tensor_copy)
+            if step == 3:
                 for unit in late:
                     if unit[2]:
                         unit[2]()
-            if 0 <= step - 1 - 2 < len(late_tests):
-                late_tests[step - 1 - 2]()
-            if late_tests and step == 1 + 2 + len(late_tests):
+            if 0 <= step - 3 - 1 < len(late_tests):
+                late_tests[step - 3 - 1]()
+            if late_tests and step == 3 + 1 + len(late_tests):
                 row_weights(B - 1)
             if tile_at(step + LEAD_DIAGONAL):
                 diagonal(step + LEAD_DIAGONAL)
+        m = ROW_TILES // GROUP - 1
+        last = ROW_TILES - 1
+        turn(last, 0)
+        quantise(last - 1)
+        regroup(last, nc.vector.tensor_copy, slice(0, 1))
+        turn(last, 1)
+        regroup(last, nc.scalar.copy, slice(1, 2))
+        sum_rows(m, nc.vector)
+        quantise(last, [0])
+        e_times_v(m, range(GROUP - 1))
+        nc.vector.reciprocal(out=tiles["weight", m][:], in_=tiles["weight", m][:])
+        quantise(last, [1])
+        weigh_rows(m, nc.vector)
+        e_times_v(m, [GROUP - 1])
+        finish(m, 0, GROUP - 1)
+        finish(m, GROUP - 1, GROUP)

import math
from contextlib import ExitStack

import concourse.mybir as mybir
from concourse.masks import make_identity

F32 = mybir.dt.float32
BF16 = mybir.dt.bfloat16
U32 = mybir.dt.uint32
U8 = mybir.dt.uint8
I32 = mybir.dt.int32
FP8X4 = mybir.dt.float8_e4m3fn_x4
ALU = mybir.AluOpType
ACT = mybir.ActivationFunctionType
AX = mybir.AxisListType

B, T, D, H = 4, 1024, 512, 4
DH = D // H
P = 128
PACK = 4
K_PASS = P * PACK
TILES = T // P
PASSES = T // K_PASS
BANK = 512
BANKS_PER_ROW = T // BANK
TILES_PER_BANK = BANK // P
GROUP = BANK // DH
ROW_TILES = B * H * TILES
HEADS = B * H

SCALE = 1.0 / math.sqrt(DH)
ABSENT_KEY = (-(2.0**32) + 1.0) / SCALE
PAST_KEY = -round(10000.0 / SCALE * 128.0) / 128.0
MAGNITUDE_BITS = 0x7FFF7FFF

LAG_MAX = 1
LAG_EXP = 2
LAG_TURN = 3
LAG_QUANTISE = 4
LAG_E_TIMES_V = 5
LAG_SUM = 3
LAG_INVERT = 4
LAG_WEIGH = 4
LAG_FINISH = 5
LEAD_DIAGONAL = 2
assert BANKS_PER_ROW == PASSES

FLOPS = 2 * B * T * D * D + 2 * 2 * B * H * T * T * DH


def tile_multiheadattention_pa_t_kernel(tc, Q, K, x, Wv, mask, out):
    nc = tc.nc
    with ExitStack() as ctx:
        const = ctx.enter_context(tc.tile_pool(name="const", bufs=1))
        keep = ctx.enter_context(tc.tile_pool(name="keep", bufs=1))
        loads = ctx.enter_context(tc.tile_pool(name="loads", bufs=2))
        work = ctx.enter_context(tc.tile_pool(name="work", bufs=2))
        rows = ctx.enter_context(tc.tile_pool(name="rows", bufs=3))
        groups = ctx.enter_context(tc.tile_pool(name="groups", bufs=3))
        ps_s = ctx.enter_context(tc.psum_pool(name="ps_s", bufs=6))
        ps_r = ctx.enter_context(tc.psum_pool(name="ps_r", bufs=2))
        ctx.enter_context(tc.manual_schedule())

        tiles = {}

        def load_tokens(b, parts):
            x_sb = loads.tile([P, TILES, D], BF16, name="x_sb")
            step = TILES // 2 // parts
            for n in range(parts):
                nc.sync.dma_start(
                    out=x_sb[:, 2 * n * step : 2 * (n + 1) * step, :].rearrange("p (a e) d -> p a (e d)", e=2),
                    in_=x[b].rearrange("(a p e) d -> p a (e d)", p=P, e=2)[:, n * step : (n + 1) * step, :],
                )
            tiles["x", b] = x_sb

        def load_rows(name, source, b):
            row_tile = loads.tile([P, TILES, D], BF16, name=name + "_sb")
            nc.sync.dma_start(out=row_tile[:], in_=source[b].rearrange("(c p) d -> p c d", p=P))
            tiles[name, b] = row_tile

        load_tokens(0, 4)
        w_sb = const.tile([P, H, D], BF16, name="w_sb")
        nc.sync.dma_start(out=w_sb[:], in_=Wv.rearrange("(h p) i -> p h i", p=P))
        load_rows("k", K, 0)
        mask_rows = const.tile([P, P], BF16, name="mask_rows")
        nc.vector.memset(mask_rows[:], 0.0)
        nc.sync.dma_start(out=mask_rows[0 : B * TILES, :], in_=mask.rearrange("b (r p) -> (b r) p", p=P))
        load_rows("q", Q, 0)
        load_rows("k", K, 1)
        load_tokens(1, 1)
        load_rows("q", Q, 1)

        ident_f = const.tile([P, P], F32, name="ident_f")
        make_identity(nc, ident_f[:])
        ident_b = const.tile([P, P], BF16, name="ident_b")
        make_identity(nc, ident_b[:])

        past_t = const.tile([P, P], F32, name="past_t")
        nc.gpsimd.memset(past_t[:], 0.0)
        nc.gpsimd.affine_select(
            out=past_t[:],
            in_=past_t[:],
            pattern=[[-1, P]],
            compare_op=ALU.is_gt,
            fill=PAST_KEY,
            base=0,
            channel_multiplier=1,
        )
        token_mask = const.tile([P, B, TILES], F32, name="token_mask")
        w_grouped = const.tile([P, H * P * PACK], BF16, name="w_grouped", align_bytes=64)
        w_codes = const.tile([P, H * P], U32, name="w_codes", align_bytes=64)
        w_scales = const.tile([P, H * P], U8, name="w_scales", align_bytes=64)

        q_t = keep.tile([P, B, H, T], BF16, name="q_t")
        k_t = keep.tile([P, B, H, T], BF16, name="k_t")
        v_codes = keep.tile([P, B, H * PASSES * DH], U32, name="v_codes", align_bytes=64)
        v_scales = keep.tile([P, B, H * PASSES * DH], U8, name="v_scales", align_bytes=64)
        later_key = keep.tile([P, B, TILES * H], F32, name="later_key")
        past_key = keep.tile([P, B, TILES * H], F32, name="past_key")
        row_on = keep.tile([P, B, TILES, H], F32, name="row_on")

        def bank(shape, dtype, name, turn_bank):
            if turn_bank:
                return ps_r.tile(shape, dtype, name=name, tag="r")
            return ps_s.tile(shape, dtype, name=name, tag="s")

        def words_unit(sources, grouped, codes, scales):
            made = {}

            def first(turn_bank):
                turned = bank([P, 2, 2, P], F32, "turned", turn_bank)
                for s in range(2):
                    words = sources[s].bitcast(F32)
                    for u in range(2):
                        nc.tensor.transpose(
                            out=turned[:, s, u, :], in_=words[:, u * P : (u + 1) * P], identity=ident_f[:]
                        )
                made["turned"] = turned

            def second(copy):
                copy(
                    out=grouped.bitcast(F32).rearrange("p (s r u) -> p s r u", s=2, u=2),
                    in_=made["turned"][:].rearrange("p s u r -> p s r u"),
                )

            def third():
                nc.vector.quantize_mx(out=codes.bitcast(FP8X4), scales=scales, in_=grouped)

            return first, second, third

        def weight_unit(pair):
            cols = slice(2 * pair * P, 2 * (pair + 1) * P)
            return words_unit(
                [w_sb[:, 2 * pair, :], w_sb[:, 2 * pair + 1, :]],
                w_grouped[:, 2 * pair * P * PACK : 2 * (pair + 1) * P * PACK],
                w_codes[:, cols],
                w_scales[:, cols],
            )

        def token_unit(b, pair):
            if pair == 0:
                tiles["xg", b] = work.tile([P, TILES * P * PACK], BF16, name="x_grouped", align_bytes=64)
                tiles["xc", b] = work.tile([P, TILES * P], U32, name="x_codes", align_bytes=64)
                tiles["xs", b] = work.tile([P, TILES * P], U8, name="x_scales", align_bytes=64)
            x_sb = tiles["x", b]
            cols = slice(2 * pair * P, 2 * (pair + 1) * P)
            return words_unit(
                [x_sb[:, 2 * pair, :], x_sb[:, 2 * pair + 1, :]],
                tiles["xg", b][:, 2 * pair * P * PACK : 2 * (pair + 1) * P * PACK],
                tiles["xc", b][:, cols],
                tiles["xs", b][:, cols],
            )

        def head_unit(b, h, name, turned_sb):
            made = {}

            def first(turn_bank):
                turned = bank([P, T], BF16, "turned_head", turn_bank)
                for c in range(TILES):
                    nc.tensor.transpose(
                        out=turned[:, c * P : (c + 1) * P],
                        in_=tiles[name, b][:, c, h * DH : (h + 1) * DH],
                        identity=ident_b[:],
                    )
                made["turned"] = turned

            def second(copy):
                copy(out=turned_sb[:, b, h, :], in_=made["turned"][:])

            return first, second, None

        def value_unit(b, h, g):
            made = {}

            def first(turn_bank):
                v_ps = bank([P, PACK, DH], F32, "v_ps", turn_bank)
                for t in range(PACK):
                    s = PACK * g + t
                    nc.tensor.matmul_mx(
                        out=v_ps[:, t, :],
                        lhsT=tiles["xc", b][:, s * P : (s + 1) * P].bitcast(FP8X4),
                        lhsT_scale=tiles["xs", b][:, s * P : (s + 1) * P],
                        rhs=w_codes[:, h * DH : (h + 1) * DH].bitcast(FP8X4),
                        rhs_scale=w_scales[:, h * DH : (h + 1) * DH],
                        start=True,
                        stop=True,
                    )
                made["v"] = v_ps

            def second(copy):
                if g == 0:
                    tiles["vg", b, h] = work.tile([P, PASSES * DH * PACK], BF16, name="v_grouped", align_bytes=64)
                copy(
                    out=tiles["vg", b, h][:, g * DH * PACK : (g + 1) * DH * PACK].rearrange("p (d t) -> p d t", t=PACK),
                    in_=made["v"][:].rearrange("p t d -> p d t"),
                )

            def third():
                codes = slice(h * PASSES * DH, (h + 1) * PASSES * DH)
                nc.vector.quantize_mx(
                    out=v_codes[:, b, codes].bitcast(FP8X4), scales=v_scales[:, b, codes], in_=tiles["vg", b, h][:]
                )

            return first, second, third if g == PASSES - 1 else None

        def zero_test(b, name, half):
            columns = TILES // 2 * H
            made = {}

            def first_or():
                words = tiles[name, b][:, half * TILES // 2 : (half + 1) * TILES // 2, :]
                words = words.rearrange("p c d -> p (c d)").bitcast(I32).rearrange("p (n w) -> p n w", w=DH // 2)
                made["32"] = work.tile([P, columns, DH // 4], I32, name="or_32")
                nc.vector.tensor_tensor(
                    out=made["32"][:], in0=words[:, :, 0 : DH // 4], in1=words[:, :, DH // 4 :], op=ALU.bitwise_or
                )

            def second_or():
                words = made["32"]
                made["16"] = work.tile([P, columns, DH // 8], I32, name="or_16")
                nc.vector.tensor_tensor(
                    out=made["16"][:], in0=words[:, :, 0 : DH // 8], in1=words[:, :, DH // 8 :], op=ALU.bitwise_or
                )

            def drop_signs():
                made["bits"] = work.tile([P, columns, DH // 8], I32, name="bits")
                nc.vector.tensor_scalar(
                    out=made["bits"][:], in0=made["16"][:], scalar1=MAGNITUDE_BITS, scalar2=None, op0=ALU.bitwise_and
                )

            def largest():
                if half == 0:
                    tiles["largest", b, name] = work.tile([P, TILES * H], F32, name="largest_" + name)
                nc.vector.tensor_reduce(
                    out=tiles["largest", b, name][:, half * columns : (half + 1) * columns],
                    in_=made["bits"][:],
                    axis=AX.X,
                    op=ALU.max,
                )

            return [first_or, second_or, drop_signs, largest]

        def absent_keys(b):
            nc.gpsimd.tensor_scalar(
                out=later_key[:, b, :],
                in0=tiles["largest", b, "k"][:],
                scalar1=0.0,
                scalar2=ABSENT_KEY,
                op0=ALU.is_equal,
                op1=ALU.mult,
            )

        def past_keys(b):
            nc.gpsimd.tensor_scalar(
                out=past_key[:, b, :],
                in0=later_key[:, b, :],
                scalar1=PAST_KEY,
                scalar2=1.0,
                op0=ALU.add,
                op1=ALU.mult,
            )

        def row_weights(b):
            nc.vector.scalar_tensor_tensor(
                out=row_on[:, b, :, :],
                in0=tiles["largest", b, "q"][:].rearrange("p (c h) -> p c h", h=H),
                scalar=0.0,
                in1=token_mask[:, b, :].unsqueeze(2).to_broadcast([P, TILES, H]),
                op0=ALU.is_gt,
                op1=ALU.mult,
            )

        def where(i):
            return i // (H * TILES), (i // TILES) % H, i % TILES

        def diagonal(i):
            b, h, r = where(i)
            on_diagonal = rows.tile([P, P], F32, name="on_diagonal")
            nc.gpsimd.tensor_scalar(
                out=on_diagonal[:],
                in0=past_t[:],
                scalar1=later_key[:, b, r * H + h : r * H + h + 1],
                scalar2=1.0,
                op0=ALU.add,
                op1=ALU.mult,
            )
            tiles["diagonal", i] = on_diagonal

        def products(i, k):
            b, h, r = where(i)
            s_ps = ps_s.tile([P, BANK], F32, name="s_ps", tag="s")
            nc.tensor.matmul(
                out=s_ps[:],
                lhsT=q_t[:, b, h, r * P : (r + 1) * P],
                rhs=k_t[:, b, h, k * BANK : (k + 1) * BANK],
                start=True,
                stop=False,
            )
            tiles["s", i, k] = s_ps

        def addends(i):
            b, h, r = where(i)
            for c in range(TILES):
                k, c4 = c // TILES_PER_BANK, c % TILES_PER_BANK
                if c == r:
                    addend = tiles["diagonal", i][:]
                else:
                    column = past_key if c < r else later_key
                    addend = column[:, b, c * H + h : c * H + h + 1].to_broadcast([P, P])
                nc.tensor.matmul(
                    out=tiles["s", i, k][:, c4 * P : (c4 + 1) * P],
                    lhsT=addend,
                    rhs=ident_f[:],
                    start=False,
                    stop=(c4 == TILES_PER_BANK - 1),
                    is_transpose=True,
                )

        def bank_maxima(i):
            bank_max = rows.tile([P, BANKS_PER_ROW], F32, name="bank_max")
            for k in range(BANKS_PER_ROW):
                nc.vector.tensor_reduce(out=bank_max[:, k : k + 1], in_=tiles["s", i, k][:], axis=AX.X, op=ALU.max)
            tiles["max", i] = bank_max

        def row_shift(i):
            shift = rows.tile([P, 1], F32, name="shift")
            bank_max = tiles["max", i]
            nc.vector.tensor_scalar(
                out=shift[:],
                in0=bank_max[:, 0:1],
                scalar1=bank_max[:, 1:2],
                scalar2=-SCALE,
                op0=ALU.max,
                op1=ALU.mult,
            )
            tiles["shift", i] = shift

        def exponentials(i):
            if i % GROUP == 0:
                tiles["sums", i // GROUP] = groups.tile([P, GROUP, BANKS_PER_ROW], F32, name="row_sums")
            e_sb = rows.tile([P, T], BF16, name="e_sb")
            shift = tiles["shift", i]
            for k in range(BANKS_PER_ROW):
                nc.scalar.activation(
                    out=e_sb[:, k * BANK : (k + 1) * BANK],
                    in_=tiles["s", i, k][:],
                    func=ACT.Exp,
                    bias=shift[:],
                    scale=SCALE,
                    accum_out=tiles["sums", i // GROUP][:, i % GROUP, k : k + 1],
                )
            tiles["e", i] = e_sb

        def turn(i, g):
            if g == 0:
                tiles["e_t", i] = ps_r.tile([P, PASSES, 2, P], F32, name="e_t", tag="r")
            e_words = tiles["e", i][:].bitcast(F32)
            for u in range(2):
                w = 2 * g + u
                nc.tensor.transpose(
                    out=tiles["e_t", i][:, g, u, :], in_=e_words[:, w * P : (w + 1) * P], identity=ident_f[:]
                )

        def regroup(i, copy, passes=slice(0, PASSES)):
            if ("grouped", i) not in tiles:
                tiles["grouped", i] = rows.tile([P, PASSES * P * PACK], BF16, name="e_grouped", align_bytes=64)
            copy(
                out=tiles["grouped", i][:].bitcast(F32).rearrange("p (g q u) -> p g q u", g=PASSES, u=2)[:, passes],
                in_=tiles["e_t", i][:].rearrange("p g u q -> p g q u")[:, passes],
            )

        def quantise(i, passes=range(PASSES)):
            if i % GROUP == 0:
                tiles["codes", i // GROUP] = groups.tile(
                    [P, GROUP * PASSES * P], U32, name="e_codes", align_bytes=64
                )
                tiles["scales", i // GROUP] = groups.tile(
                    [P, GROUP * PASSES * P], U8, name="e_scales", align_bytes=64
                )
            first, last = passes[0], passes[-1] + 1
            cols = slice((i % GROUP * PASSES + first) * P, (i % GROUP * PASSES + last) * P)
            nc.vector.quantize_mx(
                out=tiles["codes", i // GROUP][:, cols].bitcast(FP8X4),
                scales=tiles["scales", i // GROUP][:, cols],
                in_=tiles["grouped", i][:, first * P * PACK : last * P * PACK],
            )

        def sum_rows(m, engine):
            weight = groups.tile([P, GROUP], F32, name="weight")
            sums = tiles["sums", m]
            engine.tensor_tensor(out=weight[:], in0=sums[:, :, 0], in1=sums[:, :, 1], op=ALU.add)
            tiles["weight", m] = weight

        def invert_sums(m):
            nc.vector.reciprocal(out=tiles["weight", m][:], in_=tiles["weight", m][:])

        def weigh_rows(m, engine):
            b, h, r = where(m * GROUP)
            engine.tensor_tensor(
                out=tiles["weight", m][:], in0=tiles["weight", m][:], in1=row_on[:, b, r : r + GROUP, h], op=ALU.mult
            )

        def e_times_v(m, members=range(GROUP)):
            b, h, r = where(m * GROUP)
            o_ps = bank([P, len(members), DH], F32, "o_ps", members[0] == 0)
            tiles["o", m, members[0]] = o_ps
            e_codes = tiles["codes", m]
            e_scales = tiles["scales", m]
            for n in members:
                for g in range(PASSES):
                    e_cols = slice((n * PASSES + g) * P, (n * PASSES + g + 1) * P)
                    v_cols = slice((h * PASSES + g) * DH, (h * PASSES + g + 1) * DH)
                    nc.tensor.matmul_mx(
                        out=o_ps[:, n - members[0], :],
                        lhsT=e_codes[:, e_cols].bitcast(FP8X4),
                        lhsT_scale=e_scales[:, e_cols],
                        rhs=v_codes[:, b, v_cols].bitcast(FP8X4),
                        rhs_scale=v_scales[:, b, v_cols],
                        start=(g == 0),
                        stop=(g == PASSES - 1),
                    )

        def finish(m, first=0, last=GROUP):
            b, h, r = where(m * GROUP)
            o_sb = groups.tile([P, GROUP, DH], F32, name="o_sb")
            nc.vector.tensor_tensor(
                out=o_sb[:, first:last, :],
                in0=tiles["o", m, first][:],
                in1=tiles["weight", m][:, first:last].unsqueeze(2).to_broadcast([P, last - first, DH]),
                op=ALU.mult,
            )
            nc.sync.dma_start(
                out=out[b].rearrange("(r p) d -> p r d", p=P)[:, r + first : r + last, h * DH : (h + 1) * DH],
                in_=o_sb[:, first:last, :],
            )

        def tile_at(i):
            return 0 <= i < ROW_TILES

        def group_ends_at(i):
            return tile_at(i) and i % GROUP == GROUP - 1
        def whole_group_ends_at(i):
            return group_ends_at(i) and i != ROW_TILES - 1

        unit_count = [0]

        def fill(unit):
            unit[0](unit_count[0] % 4 == 3)
            unit_count[0] = unit_count[0] + 1

        def empty(unit, on_vector):
            unit[1](nc.vector.tensor_copy if on_vector else nc.scalar.copy)

        tokens = [token_unit(0, pair) for pair in range(TILES // 2)]
        weights = [weight_unit(pair) for pair in range(H // 2)]
        head_keys = [head_unit(0, h, "k", k_t) for h in range(H)]
        for unit in tokens + weights:
            fill(unit)
        for n in range(TILES // 2):
            empty(tokens[n], n % 2)
        for unit in tokens:
            unit[2]()
        for n in range(H // 2):
            empty(weights[n], n % 2)
        for unit in head_keys:
            fill(unit)
            empty(unit, False)
        for unit in weights:
            unit[2]()
        for steps in zip(zero_test(0, "k", 0), zero_test(0, "k", 1)):
            for test_step in steps:
                test_step()
        mask_ps = ps_r.tile([P, P], BF16, name="mask_ps", tag="r")
        nc.tensor.transpose(out=mask_ps[:], in_=mask_rows[:], identity=ident_b[:])
        nc.vector.tensor_copy(out=token_mask[:].rearrange("p b r -> p (b r)"), in_=mask_ps[:, 0 : B * TILES])
        absent_keys(0)

        quantisers = []
        chores = [lambda: past_keys(0)]
        late = []
        late_tests = []
        for b in range(B):
            for h in range(H):
                if h == 0 and 1 <= b < B - 1:
                    load_rows("k", K, b + 1)
                    load_tokens(b + 1, 1)
                    load_rows("q", Q, b + 1)
                queries = [head_unit(b, h, "q", q_t)]
                values = [value_unit(b, h, 0), value_unit(b, h, 1)]
                following = [head_unit(b + 1, h, "k", k_t), token_unit(b + 1, h)] if b + 1 < B else []
                group = queries + following + values
                if h % 2 == 0:
                    test = zero_test(b, "q", h // 2)
                elif b + 1 < B:
                    test = zero_test(b + 1, "k", h // 2)
                else:
                    test = []
                if b == B - 1 and h >= 3:
                    late = late + group
                    late_tests = late_tests + test
                    continue
                for n in range(3):
                    if n < len(test):
                        test[n]()
                    if n < len(quantisers):
                        quantisers[n]()
                quantisers = []
                for unit in group:
                    fill(unit)
                    empty(unit, following and unit is following[-1] and h % 2 == 1)
                    if unit[2]:
                        quantisers = quantisers + [unit[2]]
                if chores:
                    chores[0]()
                    chores = chores[1:]
                if test:
                    test[3]()
                if h == 2:
                    chores = chores + [lambda batch=b: row_weights(batch)]
                if h == 3 and b + 1 < B:
                    chores = chores + [lambda batch=b + 1: absent_keys(batch), lambda batch=b + 1: past_keys(batch)]
        for quantiser in quantisers:
            quantiser()
        for chore in chores:
            chore()
        def on_vector(i):
            return i % 8 == 2 or i == ROW_TILES - 2

        for i in range(LEAD_DIAGONAL):
            diagonal(i)
        for step in range(ROW_TILES + LAG_EXP):
            if tile_at(step):
                products(step, 0)
            if whole_group_ends_at(step - LAG_E_TIMES_V):
                e_times_v((step - LAG_E_TIMES_V) // GROUP)
            if tile_at(step):
                products(step, 1)
            for k in range(PASSES):
                if tile_at(step - LAG_TURN):
                    turn(step - LAG_TURN, k)
            if tile_at(step):
                addends(step)
            for n in range(len(late)):
                if step == (0, 1, 1)[n]:
                    late[n][0](True)
                    empty(late[n], False)
            if tile_at(step - LAG_EXP):
                exponentials(step - LAG_EXP)
            if tile_at(step - LAG_TURN) and not on_vector(step - LAG_TURN):
                regroup(step - LAG_TURN, nc.scalar.copy)
            if whole_group_ends_at(step - LAG_INVERT):
                invert_sums((step - LAG_INVERT) // GROUP)
            if whole_group_ends_at(step - LAG_WEIGH):
                weigh_rows((step - LAG_WEIGH) // GROUP, nc.gpsimd)
            if tile_at(step - LAG_MAX):
                bank_maxima(step - LAG_MAX)
            if whole_group_ends_at(step - LAG_FINISH):
                finish((step - LAG_FINISH) // GROUP)
            if whole_group_ends_at(step - LAG_SUM):
                sum_rows((step - LAG_SUM) // GROUP, nc.gpsimd)
            if tile_at(step - LAG_QUANTISE):
                quantise(step - LAG_QUANTISE)
            if tile_at(step - LAG_MAX):
                row_shift(step - LAG_MAX)
            if tile_at(step - LAG_TURN) and on_vector(step - LAG_TURN):
                regroup(step - LAG_TURN, nc.vector.tensor_copy)
            if step == 3:
                for unit in late:
                    if unit[2]:
                        unit[2]()
            if 0 <= step - 3 - 1 < len(late_tests):
                late_tests[step - 3 - 1]()
            if late_tests and step == 3 + 1 + len(late_tests):
                row_weights(B - 1)
            if tile_at(step + LEAD_DIAGONAL):
                diagonal(step + LEAD_DIAGONAL)
        m = ROW_TILES // GROUP - 1
        last = ROW_TILES - 1
        turn(last, 0)
        quantise(last - 1)
        regroup(last, nc.vector.tensor_copy, slice(0, 1))
        turn(last, 1)
        regroup(last, nc.scalar.copy, slice(1, 2))
        sum_rows(m, nc.vector)
        quantise(last, [0])
        e_times_v(m, range(GROUP - 1))
        nc.vector.reciprocal(out=tiles["weight", m][:], in_=tiles["weight", m][:])
        quantise(last, [1])
        weigh_rows(m, nc.vector)
        e_times_v(m, [GROUP - 1])
        finish(m, 0, GROUP - 1)
        finish(m, GROUP - 1, GROUP)
